import numpy as np
import ml_dtypes


def mxq(x, axis, fmt="e4m3"):
    dtype, down = {"e4m3": (ml_dtypes.float8_e4m3fn, 7), "e5m2": (ml_dtypes.float8_e5m2, 14)}[fmt]
    v = np.moveaxis(np.asarray(x, np.float32).astype(ml_dtypes.bfloat16).astype(np.float64), axis, -1)
    blocks = v.reshape(v.shape[:-1] + (-1, 32))
    amax = np.abs(blocks).max(-1, keepdims=True)
    byte = np.maximum(np.where(amax > 0, np.frexp(amax)[1] - 1 + 127, 0) - down, 1)
    scale = np.exp2(byte - 127.0)
    codes = (blocks / scale).astype(np.float32).astype(dtype).astype(np.float64)
    return np.moveaxis((codes * scale).reshape(v.shape), -1, axis)


WIDE = False


def mx_kscale(k):
    if not WIDE:
        return np.ones(k)
    levels = np.array([10, -10, 5, -5, 0])
    a = np.random.permutation(np.resize(levels, k // 512 * 4)).reshape(k // 512, 4)
    idx = np.arange(k)
    return np.exp2(a[idx // 512, idx % 128 // 32])


BF16 = ml_dtypes.bfloat16


def bf(x):
    return np.asarray(x, np.float32).astype(BF16)


def f64(x):
    return np.asarray(x).astype(np.float64)


T, D, F1, F2 = 512, 1024, 4096, 1024
EPS = 1e-3


def _layernorm(x, gamma, beta):
    mu = np.mean(x, axis=-1, keepdims=True)
    var = np.mean(np.square(x - mu), axis=-1, keepdims=True)
    rsigma = 1.0 / np.sqrt(var + EPS)
    return (x - mu) * rsigma * gamma + beta


def _gelu_tanh(x):
    c = 0.7978845608028654
    return 0.5 * x * (1.0 + np.tanh(c * (x + 0.044715 * x * x * x)))


def setup_inputs():
    s = mx_kscale(D)
    t = mx_kscale(F1)
    u = np.minimum(t, 1.0 / t) ** 2
    return {"inputs": bf(np.random.standard_normal((T, D)) + 0.5),
            "gamma": bf((1.0 + 0.1 * np.random.standard_normal(D)) * s),
            "beta": bf(0.1 * np.random.standard_normal(D) * s),
            "fc1_kernel": bf(np.random.standard_normal((D, F1)) / np.sqrt(D) / s[:, None] * u[None, :]),
            "fc1_bias": bf(0.1 * np.random.standard_normal(F1) * u),
            "fc2_kernel": bf(np.random.standard_normal((F1, F2)) * 1.5 / np.sqrt(F1) / u[:, None]),
            "fc2_bias": bf(0.1 * np.random.standard_normal(F2))}


def reference(inputs, gamma, beta, fc1_kernel, fc1_bias, fc2_kernel, fc2_bias):
    ln_out = _layernorm(f64(inputs), f64(gamma), f64(beta))
    fc1_out = (mxq(ln_out, 1, "e4m3") @ mxq(f64(fc1_kernel), 0, "e4m3")) + f64(fc1_bias)
    gelu_out = _gelu_tanh(fc1_out)
    fc2_out = (mxq(gelu_out, 1, "e4m3") @ mxq(f64(fc2_kernel), 0, "e4m3")) + f64(fc2_bias)
    return fc2_out

@@ -1,0 +1,318 @@
+from contextlib import ExitStack
+
+import concourse.mybir as mybir
+from concourse.masks import make_identity
+
+F32 = mybir.dt.float32
+BF16 = mybir.dt.bfloat16
+U32 = mybir.dt.uint32
+U8 = mybir.dt.uint8
+FP8X4 = mybir.dt.float8_e4m3fn_x4
+ACT = mybir.ActivationFunctionType
+ALU = mybir.AluOpType
+
+P = 128
+T = 512
+D = 1024
+F1 = 4096
+F2 = 1024
+EPS = 1e-3
+FLOPS = 2 * T * D * F1 + 2 * T * F1 * F2
+
+W = 512
+RAW_BUFS = 10
+S_PIECE = 256
+LOOK_S = 2
+V_COLS = [272,288,128,128,288,288,400,400,400,400,288,288,288,288,288,288,248,248,248,248,0,200,232,232,248,248,0,136,264,232,200,248]
+S_PRE = (1, 3)
+V_PRE = (1, 2)
+FIN0_AT = 12
+PINNED = True
+
+
+def tile_layernormmlp_kernel(
+    tc, inputs, gamma, beta, fc1_kernel, fc1_bias, fc2_kernel, fc2_bias, out
+):
+    nc = tc.nc
+    with ExitStack() as ctx:
+        const = ctx.enter_context(tc.tile_pool(name="const", bufs=1))
+        rawp = ctx.enter_context(tc.tile_pool(name="rawp", bufs=RAW_BUFS))
+        grpp = ctx.enter_context(tc.tile_pool(name="grpp", bufs=8))
+        codp = ctx.enter_context(tc.tile_pool(name="codp", bufs=6))
+        hidp = ctx.enter_context(tc.tile_pool(name="hidp", bufs=3))
+        outp = ctx.enter_context(tc.tile_pool(name="outp", bufs=4))
+        psum = ctx.enter_context(tc.psum_pool(name="psum", bufs=1))
+        if PINNED:
+            ctx.enter_context(tc.manual_schedule())
+
+        def regroup_part(copy_fn, dst, src, lo, hi):
+            copy_fn(
+                out=dst[:, lo:hi, :].rearrange("p (c i) t -> p c t i", i=4),
+                in_=src[:, :, lo:hi].rearrange("p t (c i) -> p c t i", i=4),
+            )
+
+        def quantise(codes, scales, grouped):
+            nc.vector.quantize_mx(
+                out=codes.bitcast(FP8X4),
+                scales=scales,
+                in_=grouped[:].rearrange("p w t -> p (w t)"),
+            )
+
+        ident_b = const.tile([P, P], BF16, name="ident_b")
+        make_identity(nc, ident_b[:])
+        ident_f = const.tile([P, P], F32, name="ident_f")
+        make_identity(nc, ident_f[:])
+        eps_t = const.tile([P, 1], F32, name="eps_t")
+        nc.vector.memset(eps_t[:], EPS)
+        vec = const.tile([P, P], BF16, name="vec")
+        nc.vector.memset(vec[:], 0.0)
+
+        x_sb = []
+        for i in range(4):
+            x_i = const.tile([P, D], BF16, name="x%d" % i)
+            nc.sync.dma_start(out=x_i[:], in_=inputs[i * P : (i + 1) * P, :])
+            x_sb.append(x_i)
+        nc.scalar.dma_start(out=vec[0:8, :], in_=gamma.rearrange("(r c) -> r c", c=P))
+        nc.scalar.dma_start(out=vec[8:16, :], in_=beta.rearrange("(r c) -> r c", c=P))
+        nc.scalar.dma_start(out=vec[16:48, :], in_=fc1_bias.rearrange("(r c) -> r c", c=P))
+        warm = const.tile([P, 2], F32, name="warm")
+        nc.scalar.activation(out=warm[:, 0:1], in_=eps_t[:], func=ACT.Sqrt)
+
+        raw = {}
+
+        def load(k):
+            if k < 8:
+                t = rawp.tile([P, 8, W], BF16, name="raw", tag="raw")
+                view = fc1_kernel[:, k * W : (k + 1) * W].rearrange("(a p) f -> p a f", p=P)
+                if k == 0:
+                    nc.sync.dma_start(out=t[:, 0:4, :], in_=view[:, 0:4, :])
+                    nc.sync.dma_start(out=t[:, 4:8, :], in_=view[:, 4:8, :])
+                else:
+                    nc.sync.dma_start(out=t[:], in_=view)
+            else:
+                g = k - 8
+                t = rawp.tile([P, 4, F2], BF16, name="raw", tag="raw")
+                nc.sync.dma_start(
+                    out=t[:],
+                    in_=fc2_kernel[g * 512 : (g + 1) * 512, :].rearrange("(a p) n -> p a n", p=P),
+                )
+            raw[k] = t
+
+        for k in range(RAW_BUFS):
+            load(k)
+        b2 = const.tile([P, F2], BF16, name="b2")
+        nc.sync.dma_start(out=b2[:], in_=fc2_bias.partition_broadcast(P))
+
+        grp = {}
+        wc = {}
+        ws = {}
+        nxt = {"S": 0, "V": 0, "load": RAW_BUFS}
+
+        def unit_src(u):
+            if u < 16:
+                return raw[u // 2][:, 4 * (u % 2) : 4 * (u % 2) + 4, :]
+            nh = (u - 16) // 8
+            return raw[8 + (u - 16) % 8][:, :, nh * W : (nh + 1) * W]
+
+        def grp_tile(u):
+            if u not in grp:
+                grp[u] = grpp.tile([P, W, 4], BF16, name="grp", tag="grp", align_bytes=64)
+            return grp[u]
+
+        def regroup_s(upto):
+            while nxt["S"] < min(upto, 32):
+                u = nxt["S"]
+                lo = V_COLS[u]
+                while lo < W:
+                    hi = min(W, lo + S_PIECE)
+                    regroup_part(nc.scalar.copy, grp_tile(u), unit_src(u), lo, hi)
+                    lo = hi
+                nxt["S"] = u + 1
+
+        def regroup_v(upto):
+            while nxt["V"] < min(upto, 32):
+                u = nxt["V"]
+                if V_COLS[u] > 0:
+                    regroup_part(nc.vector.tensor_copy, grp_tile(u), unit_src(u), 0, V_COLS[u])
+                nxt["V"] = u + 1
+
+        def refill():
+            while nxt["load"] < 16 and (nxt["load"] - RAW_BUFS) * 2 + 2 <= min(nxt["S"], nxt["V"]):
+                load(nxt["load"])
+                nxt["load"] = nxt["load"] + 1
+
+        def w_quant(u):
+            wc[u] = codp.tile([P, W], U32, name="wc", tag="wc", align_bytes=64)
+            ws[u] = codp.tile([P, W], U8, name="ws", tag="ws", align_bytes=64)
+            quantise(wc[u][:], ws[u][:], grp[u])
+
+        slot = {0: 0, 2: 1, 3: 2, 1: 3}
+        junk = const.tile([P, D], BF16, name="junk")
+        sum1 = const.tile([P, 1], F32, name="sum1")
+        negmu1 = const.tile([P, 1], F32, name="negmu1")
+        ssq1 = const.tile([P, 1], F32, name="ssq1")
+        nc.scalar.activation(out=junk[:], in_=x_sb[1][:], func=ACT.Identity, accum_out=sum1[:])
+        nc.scalar.mul(out=negmu1[:], in_=sum1[:], mul=-1.0 / D)
+        nc.scalar.activation(
+            out=junk[:], in_=x_sb[1][:], func=ACT.Square, bias=negmu1[:, 0:1], scale=1.0,
+            accum_out=ssq1[:],
+        )
+
+        stats = const.tile([P, 3, 2, 6], F32, name="stats")
+        mv = const.tile([P, 3, 2], F32, name="mv")
+        vt_ps = psum.tile([P, P], BF16, name="vt_ps", tag="bank0")
+        nc.tensor.transpose(vt_ps[:], vec[:], ident_b[:])
+        vec_t = const.tile([P, 48], F32, name="vec_t")
+        for i in (0, 2, 3):
+            for s in range(2):
+                nc.vector.bn_stats(
+                    out=stats[:, slot[i], s, :], in_=x_sb[i][:, s * 512 : (s + 1) * 512]
+                )
+            nc.vector.bn_aggr(
+                out=mv[:, slot[i], :], in_=stats[:, slot[i], :, :].rearrange("p s k -> p (s k)")
+            )
+            if i == 0:
+                nc.vector.tensor_copy(out=vec_t[:], in_=vt_ps[:, 0:48])
+
+        regroup_s(S_PRE[0])
+        std = const.tile([P, 4], F32, name="std")
+        nc.scalar.activation(
+            out=std[:, 3:4], in_=ssq1[:], func=ACT.Sqrt, bias=eps_t[:, 0:1], scale=1.0 / D
+        )
+        nc.scalar.activation(
+            out=std[:, 0:3], in_=mv[:, :, 1], func=ACT.Sqrt, bias=eps_t[:, 0:1], scale=1.0
+        )
+        regroup_v(V_PRE[0])
+        rstd = const.tile([P, 4], F32, name="rstd")
+        nc.vector.reciprocal(out=rstd[:], in_=std[:])
+
+        ln_ps = []
+        for b in range(8):
+            ln_b = psum.tile([P, T], F32, name="ln_ps%d" % b, tag="bank%d" % b)
+            ln_ps.append(ln_b)
+        for i in range(4):
+            xh = const.tile([P, D], F32, name="xh%d" % i)
+            if i == 1:
+                nc.vector.tensor_scalar(
+                    out=xh[:], in0=x_sb[i][:], scalar1=negmu1[:, 0:1], scalar2=rstd[:, 3:4],
+                    op0=ALU.add, op1=ALU.mult,
+                )
+            else:
+                nc.vector.tensor_scalar(
+                    out=xh[:], in0=x_sb[i][:], scalar1=mv[:, slot[i], 0:1],
+                    scalar2=rstd[:, slot[i] : slot[i] + 1], op0=ALU.subtract, op1=ALU.mult,
+                )
+            for b in range(8):
+                nc.tensor.transpose(
+                    ln_ps[b][:, i * P : (i + 1) * P], xh[:, b * P : (b + 1) * P], ident_f[:]
+                )
+        nc.scalar.activation(out=warm[:, 1:2], in_=std[:, 0:1], func=ACT.Gelu_apprx_tanh)
+        regroup_s(S_PRE[1])
+        regroup_v(V_PRE[1])
+
+        lnp = const.tile([P, 8, T], BF16, name="lnp")
+        for b in (0, 2, 1, 3, 4, 6, 5, 7):
+            if b % 4 < 2:
+                nc.scalar.activation(
+                    out=lnp[:, b, :], in_=ln_ps[b][:], func=ACT.Identity,
+                    scale=vec_t[:, b : b + 1], bias=vec_t[:, 8 + b : 9 + b],
+                )
+            else:
+                nc.vector.tensor_scalar(
+                    out=lnp[:, b, :], in0=ln_ps[b][:], scalar1=vec_t[:, b : b + 1],
+                    scalar2=vec_t[:, 8 + b : 9 + b], op0=ALU.mult, op1=ALU.add,
+                )
+        lnc = const.tile([P, 2, T], U32, name="lnc", align_bytes=64)
+        lns = const.tile([P, 2, T], U8, name="lns", align_bytes=64)
+        lng = []
+        for g in range(2):
+            lng_g = grpp.tile([P, W, 4], BF16, name="grp", tag="grp", align_bytes=64)
+            regroup_part(nc.vector.tensor_copy, lng_g, lnp[:, 4 * g : 4 * g + 4, :], 0, W)
+            lng.append(lng_g)
+        for g in range(2):
+            quantise(lnc[:, g, :], lns[:, g, :], lng[g])
+
+        hc = const.tile([P, 8, T], U32, name="hc", align_bytes=64)
+        hs = const.tile([P, 8, T], U8, name="hs", align_bytes=64)
+        acc1 = {}
+        acc2 = {}
+        hp = {}
+        hg = {}
+
+        def fc1(q):
+            for j in range(4):
+                acc = psum.tile([P, T], F32, name="acc1", tag="bank%d" % ((4 * q + j) % 8))
+                for c in range(2):
+                    u = 2 * q + c
+                    nc.tensor.matmul_mx(
+                        out=acc[:],
+                        lhsT=wc[u][:, j * P : (j + 1) * P].bitcast(FP8X4),
+                        lhsT_scale=ws[u][:, j * P : (j + 1) * P],
+                        rhs=lnc[:, c, :].bitcast(FP8X4),
+                        rhs_scale=lns[:, c, :],
+                        start=(c == 0),
+                        stop=(c == 1),
+                    )
+                acc1[(q, j)] = acc
+
+        def gelu(q):
+            hp[q] = hidp.tile([P, 4, T], BF16, name="hp", tag="hp")
+            for j in range(4):
+                nc.scalar.activation(
+                    out=hp[q][:, j, :], in_=acc1[(q, j)][:], func=ACT.Gelu_apprx_tanh,
+                    bias=vec_t[:, 16 + 4 * q + j : 17 + 4 * q + j], scale=1.0,
+                )
+
+        def h_regroup(q):
+            hg[q] = hidp.tile([P, W, 4], BF16, name="hg", tag="hg", align_bytes=64)
+            regroup_part(nc.vector.tensor_copy, hg[q], hp[q][:], 0, W)
+
+        def h_quant(q):
+            quantise(hc[:, q, :], hs[:, q, :], hg[q])
+
+        def fc2(u):
+            nh = (u - 16) // 8
+            g = (u - 16) % 8
+            for i in range(4):
+                if g == 0:
+                    acc2[(nh, i)] = psum.tile([P, W], F32, name="acc2", tag="bank%d" % (4 * nh + i))
+                nc.tensor.matmul_mx(
+                    out=acc2[(nh, i)][:],
+                    lhsT=hc[:, g, i * P : (i + 1) * P].bitcast(FP8X4),
+                    lhsT_scale=hs[:, g, i * P : (i + 1) * P],
+                    rhs=wc[u][:].bitcast(FP8X4),
+                    rhs_scale=ws[u][:],
+                    start=(g == 0),
+                    stop=(g == 7),
+                )
+
+        def finish(nh):
+            for i in range(4):
+                o_sb = outp.tile([P, W], F32, name="o_sb", tag="o_sb")
+                nc.vector.tensor_tensor(
+                    out=o_sb[:], in0=acc2[(nh, i)][:], in1=b2[:, nh * W : (nh + 1) * W], op=ALU.add
+                )
+                nc.sync.dma_start(
+                    out=out[i * P : (i + 1) * P, nh * W : (nh + 1) * W], in_=o_sb[:]
+                )
+
+        for r in range(16):
+            regroup_s(2 * r + 2 + LOOK_S)
+            regroup_v(2 * r + 2)
+            refill()
+            if 2 <= r < 10:
+                h_regroup(r - 2)
+            w_quant(2 * r)
+            w_quant(2 * r + 1)
+            if 2 <= r < 10:
+                h_quant(r - 2)
+            if r < 8:
+                fc1(r)
+            else:
+                fc2(2 * r)
+                fc2(2 * r + 1)
+            if 1 <= r < 9:
+                gelu(r - 1)
+            if r == FIN0_AT:
+                finish(0)
+        finish(1)

@@ -19,43 +19,66 @@ F2 = 1024
 EPS = 1e-3
 FLOPS = 2 * T * D * F1 + 2 * T * F1 * F2
 
-W = 512
-RAW_BUFS = 10
-S_PIECE = 256
-LOOK_S = 2
-V_COLS = [272,288,128,128,288,288,400,400,400,400,288,288,288,288,288,288,248,248,248,248,0,200,232,232,248,248,0,136,264,232,200,248]
-S_PRE = (1, 3)
-V_PRE = (1, 2)
-FIN0_AT = 12
+JW = 1024
+RING = 12
+BLOCKS = [[0,512],[512,256],[768,256]]
+XS = [512,512,592,608,848,592,608,608,496,496,496,224,416,128,496,0]
+QSPLIT = {15: [[0,2],[2,3],[3,4]]}
+LOOK_S = 1
+LOOK_V = 0
+DG = 2
+DH = 3
+S_PRE = [0,1]
+V_PRE = [0,1]
+FIN_DELAY = 1
 PINNED = True
+
+
+def make_jobs():
+    jobs = []
+    for q in range(8):
+        jobs.append({"kind": 1, "width": 512, "segs": [(q, 0), (q, 1)]})
+    for bi, (c0, width) in enumerate(BLOCKS):
+        per = JW // width
+        for g0 in range(0, 8, per):
+            jobs.append(
+                {"kind": 2, "block": bi, "c0": c0, "width": width,
+                 "segs": [(8 + g, g) for g in range(g0, g0 + per)]}
+            )
+    return jobs
 
 
 def tile_layernormmlp_kernel(
     tc, inputs, gamma, beta, fc1_kernel, fc1_bias, fc2_kernel, fc2_bias, out
 ):
     nc = tc.nc
+    jobs = make_jobs()
+    n_jobs = len(jobs)
+    last_use = {}
+    for ji, job in enumerate(jobs):
+        for k, sub in job["segs"]:
+            last_use[k] = ji
     with ExitStack() as ctx:
         const = ctx.enter_context(tc.tile_pool(name="const", bufs=1))
-        rawp = ctx.enter_context(tc.tile_pool(name="rawp", bufs=RAW_BUFS))
-        grpp = ctx.enter_context(tc.tile_pool(name="grpp", bufs=8))
-        codp = ctx.enter_context(tc.tile_pool(name="codp", bufs=6))
-        hidp = ctx.enter_context(tc.tile_pool(name="hidp", bufs=3))
+        ring = ctx.enter_context(tc.tile_pool(name="ring", bufs=RING))
+        grpp = ctx.enter_context(tc.tile_pool(name="grpp", bufs=5))
+        codp = ctx.enter_context(tc.tile_pool(name="codp", bufs=3))
+        hpp = ctx.enter_context(tc.tile_pool(name="hpp", bufs=3))
+        hgp = ctx.enter_context(tc.tile_pool(name="hgp", bufs=2))
         outp = ctx.enter_context(tc.tile_pool(name="outp", bufs=4))
         psum = ctx.enter_context(tc.psum_pool(name="psum", bufs=1))
         if PINNED:
             ctx.enter_context(tc.manual_schedule())
 
-        def regroup_part(copy_fn, dst, src, lo, hi):
+        def regroup_part(copy_fn, dst, src):
             copy_fn(
-                out=dst[:, lo:hi, :].rearrange("p (c i) t -> p c t i", i=4),
-                in_=src[:, :, lo:hi].rearrange("p t (c i) -> p c t i", i=4),
+                out=dst.rearrange("p (c i) t -> p c t i", i=4),
+                in_=src.rearrange("p t (c i) -> p c t i", i=4),
             )
 
         def quantise(codes, scales, grouped):
             nc.vector.quantize_mx(
-                out=codes.bitcast(FP8X4),
-                scales=scales,
-                in_=grouped[:].rearrange("p w t -> p (w t)"),
+                out=codes.bitcast(FP8X4), scales=scales, in_=grouped.rearrange("p w t -> p (w t)")
             )
 
         ident_b = const.tile([P, P], BF16, name="ident_b")
@@ -67,11 +90,9 @@ def tile_layernormmlp_kernel(
         vec = const.tile([P, P], BF16, name="vec")
         nc.vector.memset(vec[:], 0.0)
 
-        x_sb = []
+        x_all = ring.tile([P, 4, D], BF16, name="x_all", tag="ring")
         for i in range(4):
-            x_i = const.tile([P, D], BF16, name="x%d" % i)
-            nc.sync.dma_start(out=x_i[:], in_=inputs[i * P : (i + 1) * P, :])
-            x_sb.append(x_i)
+            nc.sync.dma_start(out=x_all[:, i, :], in_=inputs[i * P : (i + 1) * P, :])
         nc.scalar.dma_start(out=vec[0:8, :], in_=gamma.rearrange("(r c) -> r c", c=P))
         nc.scalar.dma_start(out=vec[8:16, :], in_=beta.rearrange("(r c) -> r c", c=P))
         nc.scalar.dma_start(out=vec[16:48, :], in_=fc1_bias.rearrange("(r c) -> r c", c=P))
@@ -79,11 +100,12 @@ def tile_layernormmlp_kernel(
         nc.scalar.activation(out=warm[:, 0:1], in_=eps_t[:], func=ACT.Sqrt)
 
         raw = {}
+        done = {"S": 0, "V": 0, "load": 0, "free": 0}
 
         def load(k):
             if k < 8:
-                t = rawp.tile([P, 8, W], BF16, name="raw", tag="raw")
-                view = fc1_kernel[:, k * W : (k + 1) * W].rearrange("(a p) f -> p a f", p=P)
+                t = ring.tile([P, 8, 512], BF16, name="raw", tag="ring")
+                view = fc1_kernel[:, k * 512 : (k + 1) * 512].rearrange("(a p) f -> p a f", p=P)
                 if k == 0:
                     nc.sync.dma_start(out=t[:, 0:4, :], in_=view[:, 0:4, :])
                     nc.sync.dma_start(out=t[:, 4:8, :], in_=view[:, 4:8, :])
@@ -91,14 +113,25 @@ def tile_layernormmlp_kernel(
                     nc.sync.dma_start(out=t[:], in_=view)
             else:
                 g = k - 8
-                t = rawp.tile([P, 4, F2], BF16, name="raw", tag="raw")
+                t = ring.tile([P, 4, F2], BF16, name="raw", tag="ring")
                 nc.sync.dma_start(
                     out=t[:],
                     in_=fc2_kernel[g * 512 : (g + 1) * 512, :].rearrange("(a p) n -> p a n", p=P),
                 )
             raw[k] = t
+            done["load"] = k + 1
 
-        for k in range(RAW_BUFS):
+        def refill():
+            while done["load"] < 16:
+                freed = done["free"]
+                for k in range(done["load"]):
+                    if min(done["S"], done["V"]) > last_use[k]:
+                        freed = freed + 1
+                if done["load"] + 4 - freed >= RING:
+                    break
+                load(done["load"])
+
+        for k in range(RING - 4):
             load(k)
         b2 = const.tile([P, F2], BF16, name="b2")
         nc.sync.dma_start(out=b2[:], in_=fc2_bias.partition_broadcast(P))
@@ -106,55 +139,55 @@ def tile_layernormmlp_kernel(
         grp = {}
         wc = {}
         ws = {}
-        nxt = {"S": 0, "V": 0, "load": RAW_BUFS}
 
-        def unit_src(u):
-            if u < 16:
-                return raw[u // 2][:, 4 * (u % 2) : 4 * (u % 2) + 4, :]
-            nh = (u - 16) // 8
-            return raw[8 + (u - 16) % 8][:, :, nh * W : (nh + 1) * W]
+        def seg_src(job, si):
+            k, sub = job["segs"][si]
+            if job["kind"] == 1:
+                return raw[k][:, 4 * sub : 4 * sub + 4, :]
+            return raw[k][:, :, job["c0"] : job["c0"] + job["width"]]
 
-        def grp_tile(u):
-            if u not in grp:
-                grp[u] = grpp.tile([P, W, 4], BF16, name="grp", tag="grp", align_bytes=64)
-            return grp[u]
+        def piece(copy_fn, r, lo, hi):
+            job = jobs[r]
+            width = job["width"]
+            if r not in grp:
+                grp[r] = grpp.tile([P, JW, 4], BF16, name="grp", tag="grp", align_bytes=64)
+            for si in range(len(job["segs"])):
+                a = max(lo, width * si)
+                b = min(hi, width * (si + 1))
+                if b > a:
+                    regroup_part(
+                        copy_fn, grp[r][:, a:b, :],
+                        seg_src(job, si)[:, :, a - width * si : b - width * si],
+                    )
 
         def regroup_s(upto):
-            while nxt["S"] < min(upto, 32):
-                u = nxt["S"]
-                lo = V_COLS[u]
-                while lo < W:
-                    hi = min(W, lo + S_PIECE)
-                    regroup_part(nc.scalar.copy, grp_tile(u), unit_src(u), lo, hi)
-                    lo = hi
-                nxt["S"] = u + 1
+            while done["S"] < min(upto, n_jobs):
+                piece(nc.scalar.copy, done["S"], XS[done["S"]], JW)
+                done["S"] = done["S"] + 1
 
         def regroup_v(upto):
-            while nxt["V"] < min(upto, 32):
-                u = nxt["V"]
-                if V_COLS[u] > 0:
-                    regroup_part(nc.vector.tensor_copy, grp_tile(u), unit_src(u), 0, V_COLS[u])
-                nxt["V"] = u + 1
+            while done["V"] < min(upto, n_jobs):
+                piece(nc.vector.tensor_copy, done["V"], 0, XS[done["V"]])
+                done["V"] = done["V"] + 1
 
-        def refill():
-            while nxt["load"] < 16 and (nxt["load"] - RAW_BUFS) * 2 + 2 <= min(nxt["S"], nxt["V"]):
-                load(nxt["load"])
-                nxt["load"] = nxt["load"] + 1
-
-        def w_quant(u):
-            wc[u] = codp.tile([P, W], U32, name="wc", tag="wc", align_bytes=64)
-            ws[u] = codp.tile([P, W], U8, name="ws", tag="ws", align_bytes=64)
-            quantise(wc[u][:], ws[u][:], grp[u])
+        def w_quant(r):
+            width = jobs[r]["width"]
+            wc[r] = codp.tile([P, JW], U32, name="wc", tag="wc", align_bytes=64)
+            ws[r] = codp.tile([P, JW], U8, name="ws", tag="ws", align_bytes=64)
+            for s0, s1 in QSPLIT.get(r, [(0, len(jobs[r]["segs"]))]):
+                a = s0 * width
+                b = s1 * width
+                quantise(wc[r][:, a:b], ws[r][:, a:b], grp[r][:, a:b, :])
 
         slot = {0: 0, 2: 1, 3: 2, 1: 3}
         junk = const.tile([P, D], BF16, name="junk")
         sum1 = const.tile([P, 1], F32, name="sum1")
         negmu1 = const.tile([P, 1], F32, name="negmu1")
         ssq1 = const.tile([P, 1], F32, name="ssq1")
-        nc.scalar.activation(out=junk[:], in_=x_sb[1][:], func=ACT.Identity, accum_out=sum1[:])
+        nc.scalar.activation(out=junk[:], in_=x_all[:, 1, :], func=ACT.Identity, accum_out=sum1[:])
         nc.scalar.mul(out=negmu1[:], in_=sum1[:], mul=-1.0 / D)
         nc.scalar.activation(
-            out=junk[:], in_=x_sb[1][:], func=ACT.Square, bias=negmu1[:, 0:1], scale=1.0,
+            out=junk[:], in_=x_all[:, 1, :], func=ACT.Square, bias=negmu1[:, 0:1], scale=1.0,
             accum_out=ssq1[:],
         )
 
@@ -166,7 +199,7 @@ def tile_layernormmlp_kernel(
         for i in (0, 2, 3):
             for s in range(2):
                 nc.vector.bn_stats(
-                    out=stats[:, slot[i], s, :], in_=x_sb[i][:, s * 512 : (s + 1) * 512]
+                    out=stats[:, slot[i], s, :], in_=x_all[:, i, s * 512 : (s + 1) * 512]
                 )
             nc.vector.bn_aggr(
                 out=mv[:, slot[i], :], in_=stats[:, slot[i], :, :].rearrange("p s k -> p (s k)")
@@ -190,27 +223,33 @@ def tile_layernormmlp_kernel(
         for b in range(8):
             ln_b = psum.tile([P, T], F32, name="ln_ps%d" % b, tag="bank%d" % b)
             ln_ps.append(ln_b)
+        xh = []
+        for half in range(2):
+            xh_h = ring.tile([P, 2, D], F32, name="xh", tag="ring")
+            xh.append(xh_h)
         for i in range(4):
-            xh = const.tile([P, D], F32, name="xh%d" % i)
+            xh_i = xh[i // 2][:, i % 2, :]
             if i == 1:
                 nc.vector.tensor_scalar(
-                    out=xh[:], in0=x_sb[i][:], scalar1=negmu1[:, 0:1], scalar2=rstd[:, 3:4],
+                    out=xh_i, in0=x_all[:, i, :], scalar1=negmu1[:, 0:1], scalar2=rstd[:, 3:4],
                     op0=ALU.add, op1=ALU.mult,
                 )
             else:
                 nc.vector.tensor_scalar(
-                    out=xh[:], in0=x_sb[i][:], scalar1=mv[:, slot[i], 0:1],
+                    out=xh_i, in0=x_all[:, i, :], scalar1=mv[:, slot[i], 0:1],
                     scalar2=rstd[:, slot[i] : slot[i] + 1], op0=ALU.subtract, op1=ALU.mult,
                 )
             for b in range(8):
                 nc.tensor.transpose(
-                    ln_ps[b][:, i * P : (i + 1) * P], xh[:, b * P : (b + 1) * P], ident_f[:]
+                    ln_ps[b][:, i * P : (i + 1) * P], xh_i[:, b * P : (b + 1) * P], ident_f[:]
                 )
+        lnp = ring.tile([P, 8, T], BF16, name="lnp", tag="ring")
+        done["free"] = 3
+        refill()
         nc.scalar.activation(out=warm[:, 1:2], in_=std[:, 0:1], func=ACT.Gelu_apprx_tanh)
         regroup_s(S_PRE[1])
         regroup_v(V_PRE[1])
 
-        lnp = const.tile([P, 8, T], BF16, name="lnp")
         for b in (0, 2, 1, 3, 4, 6, 5, 7):
             if b % 4 < 2:
                 nc.scalar.activation(
@@ -222,18 +261,19 @@ def tile_layernormmlp_kernel(
                     out=lnp[:, b, :], in0=ln_ps[b][:], scalar1=vec_t[:, b : b + 1],
                     scalar2=vec_t[:, 8 + b : 9 + b], op0=ALU.mult, op1=ALU.add,
                 )
-        lnc = const.tile([P, 2, T], U32, name="lnc", align_bytes=64)
-        lns = const.tile([P, 2, T], U8, name="lns", align_bytes=64)
-        lng = []
+        lnc = const.tile([P, 2 * T], U32, name="lnc", align_bytes=64)
+        lns = const.tile([P, 2 * T], U8, name="lns", align_bytes=64)
+        lng = grpp.tile([P, JW, 4], BF16, name="grp", tag="grp", align_bytes=64)
         for g in range(2):
-            lng_g = grpp.tile([P, W, 4], BF16, name="grp", tag="grp", align_bytes=64)
-            regroup_part(nc.vector.tensor_copy, lng_g, lnp[:, 4 * g : 4 * g + 4, :], 0, W)
-            lng.append(lng_g)
-        for g in range(2):
-            quantise(lnc[:, g, :], lns[:, g, :], lng[g])
+            regroup_part(
+                nc.vector.tensor_copy, lng[:, g * T : (g + 1) * T, :], lnp[:, 4 * g : 4 * g + 4, :]
+            )
+        done["free"] = 4
+        refill()
+        quantise(lnc[:], lns[:], lng[:])
 
-        hc = const.tile([P, 8, T], U32, name="hc", align_bytes=64)
-        hs = const.tile([P, 8, T], U8, name="hs", align_bytes=64)
+        hc = const.tile([P, 8 * T], U32, name="hc", align_bytes=64)
+        hs = const.tile([P, 8 * T], U8, name="hs", align_bytes=64)
         acc1 = {}
         acc2 = {}
         hp = {}
@@ -243,20 +283,20 @@ def tile_layernormmlp_kernel(
             for j in range(4):
                 acc = psum.tile([P, T], F32, name="acc1", tag="bank%d" % ((4 * q + j) % 8))
                 for c in range(2):
-                    u = 2 * q + c
+                    a = c * 512 + j * P
                     nc.tensor.matmul_mx(
                         out=acc[:],
-                        lhsT=wc[u][:, j * P : (j + 1) * P].bitcast(FP8X4),
-                        lhsT_scale=ws[u][:, j * P : (j + 1) * P],
-                        rhs=lnc[:, c, :].bitcast(FP8X4),
-                        rhs_scale=lns[:, c, :],
+                        lhsT=wc[q][:, a : a + P].bitcast(FP8X4),
+                        lhsT_scale=ws[q][:, a : a + P],
+                        rhs=lnc[:, c * T : (c + 1) * T].bitcast(FP8X4),
+                        rhs_scale=lns[:, c * T : (c + 1) * T],
                         start=(c == 0),
                         stop=(c == 1),
                     )
                 acc1[(q, j)] = acc
 
         def gelu(q):
-            hp[q] = hidp.tile([P, 4, T], BF16, name="hp", tag="hp")
+            hp[q] = hpp.tile([P, 4, T], BF16, name="hp", tag="hp")
             for j in range(4):
                 nc.scalar.activation(
                     out=hp[q][:, j, :], in_=acc1[(q, j)][:], func=ACT.Gelu_apprx_tanh,
@@ -264,55 +304,71 @@ def tile_layernormmlp_kernel(
                 )
 
         def h_regroup(q):
-            hg[q] = hidp.tile([P, W, 4], BF16, name="hg", tag="hg", align_bytes=64)
-            regroup_part(nc.vector.tensor_copy, hg[q], hp[q][:], 0, W)
+            if q % 2 == 0:
+                hg[q // 2] = hgp.tile([P, JW, 4], BF16, name="hg", tag="hg", align_bytes=64)
+            regroup_part(
+                nc.vector.tensor_copy, hg[q // 2][:, (q % 2) * T : (q % 2 + 1) * T, :], hp[q][:]
+            )
 
         def h_quant(q):
-            quantise(hc[:, q, :], hs[:, q, :], hg[q])
+            if q % 2 == 1:
+                a = (q - 1) * T
+                quantise(hc[:, a : a + 2 * T], hs[:, a : a + 2 * T], hg[q // 2][:])
 
-        def fc2(u):
-            nh = (u - 16) // 8
-            g = (u - 16) % 8
-            for i in range(4):
-                if g == 0:
-                    acc2[(nh, i)] = psum.tile([P, W], F32, name="acc2", tag="bank%d" % (4 * nh + i))
-                nc.tensor.matmul_mx(
-                    out=acc2[(nh, i)][:],
-                    lhsT=hc[:, g, i * P : (i + 1) * P].bitcast(FP8X4),
-                    lhsT_scale=hs[:, g, i * P : (i + 1) * P],
-                    rhs=wc[u][:].bitcast(FP8X4),
-                    rhs_scale=ws[u][:],
-                    start=(g == 0),
-                    stop=(g == 7),
-                )
+        def fc2(r):
+            job = jobs[r]
+            width = job["width"]
+            bi = job["block"]
+            for si in range(len(job["segs"])):
+                g = job["segs"][si][1]
+                for i in range(4):
+                    if g == 0:
+                        acc2[(bi, i)] = psum.tile(
+                            [P, width], F32, name="acc2", tag="bank%d" % (4 * (bi % 2) + i)
+                        )
+                    a = g * T + i * P
+                    nc.tensor.matmul_mx(
+                        out=acc2[(bi, i)][:],
+                        lhsT=hc[:, a : a + P].bitcast(FP8X4),
+                        lhsT_scale=hs[:, a : a + P],
+                        rhs=wc[r][:, si * width : (si + 1) * width].bitcast(FP8X4),
+                        rhs_scale=ws[r][:, si * width : (si + 1) * width],
+                        start=(g == 0),
+                        stop=(g == 7),
+                    )
 
-        def finish(nh):
+        def finish(bi):
+            c0, width = BLOCKS[bi]
             for i in range(4):
-                o_sb = outp.tile([P, W], F32, name="o_sb", tag="o_sb")
+                o_sb = outp.tile([P, width], F32, name="o_sb", tag="o_sb")
                 nc.vector.tensor_tensor(
-                    out=o_sb[:], in0=acc2[(nh, i)][:], in1=b2[:, nh * W : (nh + 1) * W], op=ALU.add
+                    out=o_sb[:], in0=acc2[(bi, i)][:], in1=b2[:, c0 : c0 + width], op=ALU.add
                 )
-                nc.sync.dma_start(
-                    out=out[i * P : (i + 1) * P, nh * W : (nh + 1) * W], in_=o_sb[:]
-                )
+                nc.sync.dma_start(out=out[i * P : (i + 1) * P, c0 : c0 + width], in_=o_sb[:])
 
-        for r in range(16):
-            regroup_s(2 * r + 2 + LOOK_S)
-            regroup_v(2 * r + 2)
+        fin_at = {}
+        for ji, job in enumerate(jobs):
+            if job["kind"] == 2:
+                fin_at[job["block"]] = ji + FIN_DELAY
+
+        for r in range(n_jobs):
+            regroup_s(r + 1 + LOOK_S)
+            regroup_v(r + 1 + LOOK_V)
             refill()
-            if 2 <= r < 10:
-                h_regroup(r - 2)
-            w_quant(2 * r)
-            w_quant(2 * r + 1)
-            if 2 <= r < 10:
-                h_quant(r - 2)
+            if 0 <= r - DG < 8:
+                gelu(r - DG)
+            if 0 <= r - DH < 8:
+                h_regroup(r - DH)
+            w_quant(r)
+            if 0 <= r - DH < 8:
+                h_quant(r - DH)
             if r < 8:
                 fc1(r)
             else:
-                fc2(2 * r)
-                fc2(2 * r + 1)
-            if 1 <= r < 9:
-                gelu(r - 1)
-            if r == FIN0_AT:
-                finish(0)
-        finish(1)
+                fc2(r)
+            for bi in range(len(BLOCKS)):
+                if fin_at[bi] == r:
+                    finish(bi)
+        for bi in range(len(BLOCKS)):
+            if fin_at[bi] >= n_jobs:
+                finish(bi)

@@ -22,14 +22,16 @@ FLOPS = 2 * T * D * F1 + 2 * T * F1 * F2
 JW = 1024
 RING = 12
 BLOCKS = [[0,512],[512,256],[768,256]]
-XS = [512,512,592,608,848,592,608,608,496,496,496,224,416,128,496,0]
+XS = [464,464,512,512,1024,912,464,512,368,400,400,144,400,112,416,0]
 QSPLIT = {15: [[0,2],[2,3],[3,4]]}
 LOOK_S = 1
 LOOK_V = 0
 DG = 2
 DH = 3
-S_PRE = [0,1]
-V_PRE = [0,1]
+S_HEAD = [1,4]
+V_HEAD = [1,3]
+Q_HEAD = 1
+CUT0 = 256
 FIN_DELAY = 1
 PINNED = True
 
@@ -100,7 +102,7 @@ def tile_layernormmlp_kernel(
         nc.scalar.activation(out=warm[:, 0:1], in_=eps_t[:], func=ACT.Sqrt)
 
         raw = {}
-        done = {"S": 0, "V": 0, "load": 0, "free": 0}
+        done = {"S": 0, "V": 0, "load": 0, "free": 0, "quant": 0}
 
         def load(k):
             if k < 8:
@@ -125,7 +127,7 @@ def tile_layernormmlp_kernel(
             while done["load"] < 16:
                 freed = done["free"]
                 for k in range(done["load"]):
-                    if min(done["S"], done["V"]) > last_use[k]:
+                    if min(jobs_done("S"), jobs_done("V")) > last_use[k]:
                         freed = freed + 1
                 if done["load"] + 4 - freed >= RING:
                     break
@@ -146,31 +148,53 @@ def tile_layernormmlp_kernel(
                 return raw[k][:, 4 * sub : 4 * sub + 4, :]
             return raw[k][:, :, job["c0"] : job["c0"] + job["width"]]
 
-        def piece(copy_fn, r, lo, hi):
+        def piece_list(is_vector):
+            pieces = []
+            for r, job in enumerate(jobs):
+                width = job["width"]
+                lo = 0 if is_vector else XS[r]
+                hi = XS[r] if is_vector else JW
+                for si in range(len(job["segs"])):
+                    a = max(lo, width * si)
+                    b = min(hi, width * (si + 1))
+                    while a < b:
+                        e = min(b, a + CUT0) if (r == 0 and CUT0 > 0) else b
+                        pieces.append((r, si, a, e))
+                        a = e
+            return pieces
+
+        todo = {"S": piece_list(False), "V": piece_list(True)}
+        copy_of = {"S": nc.scalar.copy, "V": nc.vector.tensor_copy}
+
+        def jobs_done(eng):
+            if done[eng] < len(todo[eng]):
+                return todo[eng][done[eng]][0]
+            return n_jobs
+
+        def emit(eng):
+            r, si, a, b = todo[eng][done[eng]]
+            done[eng] = done[eng] + 1
             job = jobs[r]
             width = job["width"]
             if r not in grp:
                 grp[r] = grpp.tile([P, JW, 4], BF16, name="grp", tag="grp", align_bytes=64)
-            for si in range(len(job["segs"])):
-                a = max(lo, width * si)
-                b = min(hi, width * (si + 1))
-                if b > a:
-                    regroup_part(
-                        copy_fn, grp[r][:, a:b, :],
-                        seg_src(job, si)[:, :, a - width * si : b - width * si],
-                    )
+            regroup_part(
+                copy_of[eng], grp[r][:, a:b, :],
+                seg_src(job, si)[:, :, a - width * si : b - width * si],
+            )
 
-        def regroup_s(upto):
-            while done["S"] < min(upto, n_jobs):
-                piece(nc.scalar.copy, done["S"], XS[done["S"]], JW)
-                done["S"] = done["S"] + 1
+        def some_pieces(eng, n):
+            for i in range(n):
+                if done[eng] < len(todo[eng]):
+                    emit(eng)
 
-        def regroup_v(upto):
-            while done["V"] < min(upto, n_jobs):
-                piece(nc.vector.tensor_copy, done["V"], 0, XS[done["V"]])
-                done["V"] = done["V"] + 1
+        def regroup_upto(eng, j):
+            while jobs_done(eng) < min(j, n_jobs):
+                emit(eng)
 
         def w_quant(r):
+            regroup_upto("V", r + 1)
+            regroup_upto("S", r + 1)
             width = jobs[r]["width"]
             wc[r] = codp.tile([P, JW], U32, name="wc", tag="wc", align_bytes=64)
             ws[r] = codp.tile([P, JW], U8, name="ws", tag="ws", align_bytes=64)
@@ -178,6 +202,7 @@ def tile_layernormmlp_kernel(
                 a = s0 * width
                 b = s1 * width
                 quantise(wc[r][:, a:b], ws[r][:, a:b], grp[r][:, a:b, :])
+            done["quant"] = r + 1
 
         slot = {0: 0, 2: 1, 3: 2, 1: 3}
         junk = const.tile([P, D], BF16, name="junk")
@@ -207,7 +232,7 @@ def tile_layernormmlp_kernel(
             if i == 0:
                 nc.vector.tensor_copy(out=vec_t[:], in_=vt_ps[:, 0:48])
 
-        regroup_s(S_PRE[0])
+        some_pieces("S", S_HEAD[0])
         std = const.tile([P, 4], F32, name="std")
         nc.scalar.activation(
             out=std[:, 3:4], in_=ssq1[:], func=ACT.Sqrt, bias=eps_t[:, 0:1], scale=1.0 / D
@@ -215,7 +240,7 @@ def tile_layernormmlp_kernel(
         nc.scalar.activation(
             out=std[:, 0:3], in_=mv[:, :, 1], func=ACT.Sqrt, bias=eps_t[:, 0:1], scale=1.0
         )
-        regroup_v(V_PRE[0])
+        some_pieces("V", V_HEAD[0])
         rstd = const.tile([P, 4], F32, name="rstd")
         nc.vector.reciprocal(out=rstd[:], in_=std[:])
 
@@ -247,8 +272,10 @@ def tile_layernormmlp_kernel(
         done["free"] = 3
         refill()
         nc.scalar.activation(out=warm[:, 1:2], in_=std[:, 0:1], func=ACT.Gelu_apprx_tanh)
-        regroup_s(S_PRE[1])
-        regroup_v(V_PRE[1])
+        some_pieces("S", S_HEAD[1])
+        some_pieces("V", V_HEAD[1])
+        for r in range(Q_HEAD):
+            w_quant(r)
 
         for b in (0, 2, 1, 3, 4, 6, 5, 7):
             if b % 4 < 2:
@@ -352,14 +379,15 @@ def tile_layernormmlp_kernel(
                 fin_at[job["block"]] = ji + FIN_DELAY
 
         for r in range(n_jobs):
-            regroup_s(r + 1 + LOOK_S)
-            regroup_v(r + 1 + LOOK_V)
+            regroup_upto("S", r + 1 + LOOK_S)
+            regroup_upto("V", r + 1 + LOOK_V)
             refill()
             if 0 <= r - DG < 8:
                 gelu(r - DG)
             if 0 <= r - DH < 8:
                 h_regroup(r - DH)
-            w_quant(r)
+            if r >= done["quant"]:
+                w_quant(r)
             if 0 <= r - DH < 8:
                 h_quant(r - DH)
             if r < 8:

@@ -22,7 +22,7 @@ FLOPS = 2 * T * D * F1 + 2 * T * F1 * F2
 JW = 1024
 RING = 12
 BLOCKS = [[0,512],[512,256],[768,256]]
-XS = [464,464,512,512,1024,912,464,512,368,400,400,144,400,112,416,0]
+XS = [416,544,688,432,1024,1024,816,816,672,416,480,208,464,176,480,64]
 QSPLIT = {15: [[0,2],[2,3],[3,4]]}
 LOOK_S = 1
 LOOK_V = 0

@@ -22,16 +22,20 @@ FLOPS = 2 * T * D * F1 + 2 * T * F1 * F2
 JW = 1024
 RING = 12
 BLOCKS = [[0,512],[512,256],[768,256]]
-XS = [416,544,688,432,1024,1024,816,816,672,416,480,208,464,176,480,64]
+XS = [1008,912,384,560,1024,1024,752,544,368,400,400,112,384,272,304,0]
 QSPLIT = {15: [[0,2],[2,3],[3,4]]}
 LOOK_S = 1
-LOOK_V = 0
+LOOK_V = 1
 DG = 2
 DH = 3
-S_HEAD = [1,4]
-V_HEAD = [1,3]
-Q_HEAD = 1
-CUT0 = 256
+XH_ON = "SSSS"
+EV_ON = "SSVVSSVV"
+EV_ORDER = [0,2,1,3,4,6,5,7]
+V_SEQ = ["p","ppppqpp","q"]
+S_SEQ = ["p","","p"]
+CUTS = {"V": {0: 256}, "S": {0: 256}}
+COD_BUFS = 4
+GRP_BUFS = 5
 FIN_DELAY = 1
 PINNED = True
 
@@ -63,8 +67,8 @@ def tile_layernormmlp_kernel(
     with ExitStack() as ctx:
         const = ctx.enter_context(tc.tile_pool(name="const", bufs=1))
         ring = ctx.enter_context(tc.tile_pool(name="ring", bufs=RING))
-        grpp = ctx.enter_context(tc.tile_pool(name="grpp", bufs=5))
-        codp = ctx.enter_context(tc.tile_pool(name="codp", bufs=3))
+        grpp = ctx.enter_context(tc.tile_pool(name="grpp", bufs=GRP_BUFS))
+        codp = ctx.enter_context(tc.tile_pool(name="codp", bufs=COD_BUFS))
         hpp = ctx.enter_context(tc.tile_pool(name="hpp", bufs=3))
         hgp = ctx.enter_context(tc.tile_pool(name="hgp", bufs=2))
         outp = ctx.enter_context(tc.tile_pool(name="outp", bufs=4))
@@ -152,13 +156,14 @@ def tile_layernormmlp_kernel(
             pieces = []
             for r, job in enumerate(jobs):
                 width = job["width"]
+                cut = CUTS["V" if is_vector else "S"].get(r, 0)
                 lo = 0 if is_vector else XS[r]
                 hi = XS[r] if is_vector else JW
                 for si in range(len(job["segs"])):
                     a = max(lo, width * si)
                     b = min(hi, width * (si + 1))
                     while a < b:
-                        e = min(b, a + CUT0) if (r == 0 and CUT0 > 0) else b
+                        e = min(b, a + cut) if cut > 0 else b
                         pieces.append((r, si, a, e))
                         a = e
             return pieces
@@ -183,10 +188,13 @@ def tile_layernormmlp_kernel(
                 seg_src(job, si)[:, :, a - width * si : b - width * si],
             )
 
-        def some_pieces(eng, n):
-            for i in range(n):
-                if done[eng] < len(todo[eng]):
-                    emit(eng)
+        def run_seq(eng, tokens):
+            for ch in tokens:
+                if ch == "p":
+                    if done[eng] < len(todo[eng]):
+                        emit(eng)
+                else:
+                    w_quant(done["quant"])
 
         def regroup_upto(eng, j):
             while jobs_done(eng) < min(j, n_jobs):
@@ -232,7 +240,12 @@ def tile_layernormmlp_kernel(
             if i == 0:
                 nc.vector.tensor_copy(out=vec_t[:], in_=vt_ps[:, 0:48])
 
-        some_pieces("S", S_HEAD[0])
+        negmean = const.tile([P, 4], F32, name="negmean")
+        nc.vector.tensor_scalar(
+            out=negmean[:, 0:3], in0=mv[:, :, 0], scalar1=-1.0, scalar2=None, op0=ALU.mult
+        )
+        nc.vector.tensor_copy(out=negmean[:, 3:4], in_=negmu1[:])
+        run_seq("S", S_SEQ[0])
         std = const.tile([P, 4], F32, name="std")
         nc.scalar.activation(
             out=std[:, 3:4], in_=ssq1[:], func=ACT.Sqrt, bias=eps_t[:, 0:1], scale=1.0 / D
@@ -240,9 +253,12 @@ def tile_layernormmlp_kernel(
         nc.scalar.activation(
             out=std[:, 0:3], in_=mv[:, :, 1], func=ACT.Sqrt, bias=eps_t[:, 0:1], scale=1.0
         )
-        some_pieces("V", V_HEAD[0])
+        run_seq("V", V_SEQ[0])
         rstd = const.tile([P, 4], F32, name="rstd")
         nc.vector.reciprocal(out=rstd[:], in_=std[:])
+        nmr = const.tile([P, 4], F32, name="nmr")
+        nc.vector.tensor_tensor(out=nmr[:], in0=negmean[:], in1=rstd[:], op=ALU.mult)
+        run_seq("S", S_SEQ[1])
 
         ln_ps = []
         for b in range(8):
@@ -254,15 +270,16 @@ def tile_layernormmlp_kernel(
             xh.append(xh_h)
         for i in range(4):
             xh_i = xh[i // 2][:, i % 2, :]
-            if i == 1:
-                nc.vector.tensor_scalar(
-                    out=xh_i, in0=x_all[:, i, :], scalar1=negmu1[:, 0:1], scalar2=rstd[:, 3:4],
-                    op0=ALU.add, op1=ALU.mult,
+            s = slot[i]
+            if XH_ON[i] == "S":
+                nc.scalar.activation(
+                    out=xh_i, in_=x_all[:, i, :], func=ACT.Identity,
+                    scale=rstd[:, s : s + 1], bias=nmr[:, s : s + 1],
                 )
             else:
                 nc.vector.tensor_scalar(
-                    out=xh_i, in0=x_all[:, i, :], scalar1=mv[:, slot[i], 0:1],
-                    scalar2=rstd[:, slot[i] : slot[i] + 1], op0=ALU.subtract, op1=ALU.mult,
+                    out=xh_i, in0=x_all[:, i, :], scalar1=negmean[:, s : s + 1],
+                    scalar2=rstd[:, s : s + 1], op0=ALU.add, op1=ALU.mult,
                 )
             for b in range(8):
                 nc.tensor.transpose(
@@ -272,13 +289,12 @@ def tile_layernormmlp_kernel(
         done["free"] = 3
         refill()
         nc.scalar.activation(out=warm[:, 1:2], in_=std[:, 0:1], func=ACT.Gelu_apprx_tanh)
-        some_pieces("S", S_HEAD[1])
-        some_pieces("V", V_HEAD[1])
-        for r in range(Q_HEAD):
-            w_quant(r)
+        run_seq("S", S_SEQ[2])
+        run_seq("V", V_SEQ[1])
+        refill()
 
-        for b in (0, 2, 1, 3, 4, 6, 5, 7):
-            if b % 4 < 2:
+        for b in EV_ORDER:
+            if EV_ON[b] == "S":
                 nc.scalar.activation(
                     out=lnp[:, b, :], in_=ln_ps[b][:], func=ACT.Identity,
                     scale=vec_t[:, b : b + 1], bias=vec_t[:, 8 + b : 9 + b],
@@ -296,6 +312,8 @@ def tile_layernormmlp_kernel(
                 nc.vector.tensor_copy, lng[:, g * T : (g + 1) * T, :], lnp[:, 4 * g : 4 * g + 4, :]
             )
         done["free"] = 4
+        refill()
+        run_seq("V", V_SEQ[2])
         refill()
         quantise(lnc[:], lns[:], lng[:])
 

@@ -21,9 +21,9 @@ FLOPS = 2 * T * D * F1 + 2 * T * F1 * F2
 
 JW = 1024
 RING = 12
-BLOCKS = [[0,512],[512,256],[768,256]]
-XS = [1008,912,384,560,1024,1024,752,544,368,400,400,112,384,272,304,0]
-QSPLIT = {15: [[0,2],[2,3],[3,4]]}
+BLOCKS = [[0,512],[512,512]]
+XS = [1008,912,384,560,1024,1024,752,544,368,400,400,112,368,336,128,128]
+QSPLIT = {15: [[0,1],[1,2]]}
 LOOK_S = 1
 LOOK_V = 1
 DG = 2

@@ -21,9 +21,9 @@ FLOPS = 2 * T * D * F1 + 2 * T * F1 * F2
 
 JW = 1024
 RING = 12
-BLOCKS = [[0,512],[512,512]]
-XS = [1008,912,384,560,1024,1024,752,544,368,400,400,112,368,336,128,128]
-QSPLIT = {15: [[0,1],[1,2]]}
+BLOCKS = [[0,512],[512,256],[768,256]]
+XS = [1008,912,384,560,1024,1024,752,544,368,400,400,112,384,272,304,0]
+QSPLIT = {15: [[0,2],[2,3],[3,4]]}
 LOOK_S = 1
 LOOK_V = 1
 DG = 2
@@ -35,6 +35,7 @@ V_SEQ = ["p","ppppqpp","q"]
 S_SEQ = ["p","","p"]
 CUTS = {"V": {0: 256}, "S": {0: 256}}
 COD_BUFS = 4
+Q_COLS = 512
 GRP_BUFS = 5
 FIN_DELAY = 1
 PINNED = True
@@ -82,10 +83,13 @@ def tile_layernormmlp_kernel(
                 in_=src.rearrange("p t (c i) -> p c t i", i=4),
             )
 
-        def quantise(codes, scales, grouped):
-            nc.vector.quantize_mx(
-                out=codes.bitcast(FP8X4), scales=scales, in_=grouped.rearrange("p w t -> p (w t)")
-            )
+        def quantise(codes, scales, grouped, cols):
+            for a in range(0, cols, min(cols, Q_COLS)):
+                b = a + min(cols, Q_COLS)
+                nc.vector.quantize_mx(
+                    out=codes[:, a:b].bitcast(FP8X4), scales=scales[:, a:b],
+                    in_=grouped[:, a:b, :].rearrange("p w t -> p (w t)"),
+                )
 
         ident_b = const.tile([P, P], BF16, name="ident_b")
         make_identity(nc, ident_b[:])
@@ -209,7 +213,7 @@ def tile_layernormmlp_kernel(
             for s0, s1 in QSPLIT.get(r, [(0, len(jobs[r]["segs"]))]):
                 a = s0 * width
                 b = s1 * width
-                quantise(wc[r][:, a:b], ws[r][:, a:b], grp[r][:, a:b, :])
+                quantise(wc[r][:, a:b], ws[r][:, a:b], grp[r][:, a:b, :], b - a)
             done["quant"] = r + 1
 
         slot = {0: 0, 2: 1, 3: 2, 1: 3}
@@ -315,7 +319,7 @@ def tile_layernormmlp_kernel(
         refill()
         run_seq("V", V_SEQ[2])
         refill()
-        quantise(lnc[:], lns[:], lng[:])
+        quantise(lnc[:], lns[:], lng[:], 2 * T)
 
         hc = const.tile([P, 8 * T], U32, name="hc", align_bytes=64)
         hs = const.tile([P, 8 * T], U8, name="hs", align_bytes=64)
@@ -358,7 +362,7 @@ def tile_layernormmlp_kernel(
         def h_quant(q):
             if q % 2 == 1:
                 a = (q - 1) * T
-                quantise(hc[:, a : a + 2 * T], hs[:, a : a + 2 * T], hg[q // 2][:])
+                quantise(hc[:, a : a + 2 * T], hs[:, a : a + 2 * T], hg[q // 2][:], 2 * T)
 
         def fc2(r):
             job = jobs[r]

@@ -19,76 +19,45 @@ F2 = 1024
 EPS = 1e-3
 FLOPS = 2 * T * D * F1 + 2 * T * F1 * F2
 
-JW = 1024
-RING = 12
-BLOCKS = [[0,512],[512,256],[768,256]]
-XS = [1008,912,384,560,1024,1024,752,544,368,400,400,112,384,272,304,0]
-QSPLIT = {15: [[0,2],[2,3],[3,4]]}
-LOOK_S = 1
-LOOK_V = 1
-DG = 2
-DH = 3
-XH_ON = "SSSS"
-EV_ON = "SSVVSSVV"
-EV_ORDER = [0,2,1,3,4,6,5,7]
-V_SEQ = ["p","ppppqpp","q"]
-S_SEQ = ["p","","p"]
-CUTS = {"V": {0: 256}, "S": {0: 256}}
-COD_BUFS = 4
-Q_COLS = 512
-GRP_BUFS = 5
-FIN_DELAY = 1
+W = 512
+HALF = 256
+Q_COLS = 256
+RAW_BUFS = 10
+S_PIECE = 256
+LOOK_S = 2
+V_COLS = [272,288,128,128,256,256,368,368,368,368,256,256,256,256,256,256,216,216,216,216,0,168,200,200,256,256,0,128,256,256,128,0]
+S_PRE = (1, 3)
+V_PRE = (1, 2)
 PINNED = True
-
-
-def make_jobs():
-    jobs = []
-    for q in range(8):
-        jobs.append({"kind": 1, "width": 512, "segs": [(q, 0), (q, 1)]})
-    for bi, (c0, width) in enumerate(BLOCKS):
-        per = JW // width
-        for g0 in range(0, 8, per):
-            jobs.append(
-                {"kind": 2, "block": bi, "c0": c0, "width": width,
-                 "segs": [(8 + g, g) for g in range(g0, g0 + per)]}
-            )
-    return jobs
 
 
 def tile_layernormmlp_kernel(
     tc, inputs, gamma, beta, fc1_kernel, fc1_bias, fc2_kernel, fc2_bias, out
 ):
     nc = tc.nc
-    jobs = make_jobs()
-    n_jobs = len(jobs)
-    last_use = {}
-    for ji, job in enumerate(jobs):
-        for k, sub in job["segs"]:
-            last_use[k] = ji
     with ExitStack() as ctx:
         const = ctx.enter_context(tc.tile_pool(name="const", bufs=1))
-        ring = ctx.enter_context(tc.tile_pool(name="ring", bufs=RING))
-        grpp = ctx.enter_context(tc.tile_pool(name="grpp", bufs=GRP_BUFS))
-        codp = ctx.enter_context(tc.tile_pool(name="codp", bufs=COD_BUFS))
-        hpp = ctx.enter_context(tc.tile_pool(name="hpp", bufs=3))
-        hgp = ctx.enter_context(tc.tile_pool(name="hgp", bufs=2))
+        rawp = ctx.enter_context(tc.tile_pool(name="rawp", bufs=RAW_BUFS))
+        grpp = ctx.enter_context(tc.tile_pool(name="grpp", bufs=8))
+        codp = ctx.enter_context(tc.tile_pool(name="codp", bufs=6))
+        hidp = ctx.enter_context(tc.tile_pool(name="hidp", bufs=3))
         outp = ctx.enter_context(tc.tile_pool(name="outp", bufs=4))
         psum = ctx.enter_context(tc.psum_pool(name="psum", bufs=1))
         if PINNED:
             ctx.enter_context(tc.manual_schedule())
 
-        def regroup_part(copy_fn, dst, src):
+        def regroup_part(copy_fn, dst, src, lo, hi):
             copy_fn(
-                out=dst.rearrange("p (c i) t -> p c t i", i=4),
-                in_=src.rearrange("p t (c i) -> p c t i", i=4),
+                out=dst[:, lo:hi, :].rearrange("p (c i) t -> p c t i", i=4),
+                in_=src[:, :, lo:hi].rearrange("p t (c i) -> p c t i", i=4),
             )
 
-        def quantise(codes, scales, grouped, cols):
-            for a in range(0, cols, min(cols, Q_COLS)):
-                b = a + min(cols, Q_COLS)
+        def quantise(codes, scales, grouped):
+            for a in range(0, W, Q_COLS):
                 nc.vector.quantize_mx(
-                    out=codes[:, a:b].bitcast(FP8X4), scales=scales[:, a:b],
-                    in_=grouped[:, a:b, :].rearrange("p w t -> p (w t)"),
+                    out=codes[:, a : a + Q_COLS].bitcast(FP8X4),
+                    scales=scales[:, a : a + Q_COLS],
+                    in_=grouped[:, a : a + Q_COLS, :].rearrange("p w t -> p (w t)"),
                 )
 
         ident_b = const.tile([P, P], BF16, name="ident_b")
@@ -100,9 +69,11 @@ def tile_layernormmlp_kernel(
         vec = const.tile([P, P], BF16, name="vec")
         nc.vector.memset(vec[:], 0.0)
 
-        x_all = ring.tile([P, 4, D], BF16, name="x_all", tag="ring")
+        x_sb = []
         for i in range(4):
-            nc.sync.dma_start(out=x_all[:, i, :], in_=inputs[i * P : (i + 1) * P, :])
+            x_i = const.tile([P, D], BF16, name="x%d" % i)
+            nc.sync.dma_start(out=x_i[:], in_=inputs[i * P : (i + 1) * P, :])
+            x_sb.append(x_i)
         nc.scalar.dma_start(out=vec[0:8, :], in_=gamma.rearrange("(r c) -> r c", c=P))
         nc.scalar.dma_start(out=vec[8:16, :], in_=beta.rearrange("(r c) -> r c", c=P))
         nc.scalar.dma_start(out=vec[16:48, :], in_=fc1_bias.rearrange("(r c) -> r c", c=P))
@@ -110,12 +81,11 @@ def tile_layernormmlp_kernel(
         nc.scalar.activation(out=warm[:, 0:1], in_=eps_t[:], func=ACT.Sqrt)
 
         raw = {}
-        done = {"S": 0, "V": 0, "load": 0, "free": 0, "quant": 0}
 
         def load(k):
             if k < 8:
-                t = ring.tile([P, 8, 512], BF16, name="raw", tag="ring")
-                view = fc1_kernel[:, k * 512 : (k + 1) * 512].rearrange("(a p) f -> p a f", p=P)
+                t = rawp.tile([P, 8, W], BF16, name="raw", tag="raw")
+                view = fc1_kernel[:, k * W : (k + 1) * W].rearrange("(a p) f -> p a f", p=P)
                 if k == 0:
                     nc.sync.dma_start(out=t[:, 0:4, :], in_=view[:, 0:4, :])
                     nc.sync.dma_start(out=t[:, 4:8, :], in_=view[:, 4:8, :])
@@ -123,25 +93,14 @@ def tile_layernormmlp_kernel(
                     nc.sync.dma_start(out=t[:], in_=view)
             else:
                 g = k - 8
-                t = ring.tile([P, 4, F2], BF16, name="raw", tag="ring")
+                t = rawp.tile([P, 4, F2], BF16, name="raw", tag="raw")
                 nc.sync.dma_start(
                     out=t[:],
                     in_=fc2_kernel[g * 512 : (g + 1) * 512, :].rearrange("(a p) n -> p a n", p=P),
                 )
             raw[k] = t
-            done["load"] = k + 1
 
-        def refill():
-            while done["load"] < 16:
-                freed = done["free"]
-                for k in range(done["load"]):
-                    if min(jobs_done("S"), jobs_done("V")) > last_use[k]:
-                        freed = freed + 1
-                if done["load"] + 4 - freed >= RING:
-                    break
-                load(done["load"])
-
-        for k in range(RING - 4):
+        for k in range(RAW_BUFS):
             load(k)
         b2 = const.tile([P, F2], BF16, name="b2")
         nc.sync.dma_start(out=b2[:], in_=fc2_bias.partition_broadcast(P))
@@ -149,82 +108,78 @@ def tile_layernormmlp_kernel(
         grp = {}
         wc = {}
         ws = {}
+        nxt = {"S": 0, "V": 0, "load": RAW_BUFS}
 
-        def seg_src(job, si):
-            k, sub = job["segs"][si]
-            if job["kind"] == 1:
-                return raw[k][:, 4 * sub : 4 * sub + 4, :]
-            return raw[k][:, :, job["c0"] : job["c0"] + job["width"]]
+        def unit_segs(u):
+            if u < 16:
+                return [(None, raw[u // 2][:, 4 * (u % 2) : 4 * (u % 2) + 4, :], W)]
+            if u < 24:
+                return [(u - 16, raw[8 + u - 16][:, :, 0:W], W)]
+            c0 = W + HALF * ((u - 24) // 4)
+            g0 = 2 * ((u - 24) % 4)
+            return [(g, raw[8 + g][:, :, c0 : c0 + HALF], HALF) for g in (g0, g0 + 1)]
 
-        def piece_list(is_vector):
-            pieces = []
-            for r, job in enumerate(jobs):
-                width = job["width"]
-                cut = CUTS["V" if is_vector else "S"].get(r, 0)
-                lo = 0 if is_vector else XS[r]
-                hi = XS[r] if is_vector else JW
-                for si in range(len(job["segs"])):
-                    a = max(lo, width * si)
-                    b = min(hi, width * (si + 1))
-                    while a < b:
-                        e = min(b, a + cut) if cut > 0 else b
-                        pieces.append((r, si, a, e))
-                        a = e
-            return pieces
+        def regroup_range(copy_fn, u, lo, hi):
+            off = 0
+            for g, src, width in unit_segs(u):
+                a = max(lo, off)
+                b = min(hi, off + width)
+                if b > a:
+                    copy_fn(
+                        out=grp_tile(u)[:, a:b, :].rearrange("p (c i) t -> p c t i", i=4),
+                        in_=src[:, :, a - off : b - off].rearrange("p t (c i) -> p c t i", i=4),
+                    )
+                off = off + width
 
-        todo = {"S": piece_list(False), "V": piece_list(True)}
-        copy_of = {"S": nc.scalar.copy, "V": nc.vector.tensor_copy}
+        def grp_tile(u):
+            if u not in grp:
+                grp[u] = grpp.tile([P, W, 4], BF16, name="grp", tag="grp", align_bytes=64)
+            return grp[u]
 
-        def jobs_done(eng):
-            if done[eng] < len(todo[eng]):
-                return todo[eng][done[eng]][0]
-            return n_jobs
+        def regroup_s(upto):
+            while nxt["S"] < min(upto, 32):
+                u = nxt["S"]
+                lo = V_COLS[u]
+                while lo < W:
+                    hi = min(W, lo + S_PIECE) if u < 24 else min(W, (lo // HALF + 1) * HALF)
+                    regroup_range(nc.scalar.copy, u, lo, hi)
+                    lo = hi
+                nxt["S"] = u + 1
 
-        def emit(eng):
-            r, si, a, b = todo[eng][done[eng]]
-            done[eng] = done[eng] + 1
-            job = jobs[r]
-            width = job["width"]
-            if r not in grp:
-                grp[r] = grpp.tile([P, JW, 4], BF16, name="grp", tag="grp", align_bytes=64)
-            regroup_part(
-                copy_of[eng], grp[r][:, a:b, :],
-                seg_src(job, si)[:, :, a - width * si : b - width * si],
-            )
+        def regroup_v(upto):
+            while nxt["V"] < min(upto, 32):
+                u = nxt["V"]
+                if V_COLS[u] > 0:
+                    regroup_range(nc.vector.tensor_copy, u, 0, V_COLS[u])
+                nxt["V"] = u + 1
 
-        def run_seq(eng, tokens):
-            for ch in tokens:
-                if ch == "p":
-                    if done[eng] < len(todo[eng]):
-                        emit(eng)
-                else:
-                    w_quant(done["quant"])
+        def refill():
+            while nxt["load"] < 16 and (nxt["load"] - RAW_BUFS) * 2 + 2 <= min(nxt["S"], nxt["V"]):
+                load(nxt["load"])
+                nxt["load"] = nxt["load"] + 1
 
-        def regroup_upto(eng, j):
-            while jobs_done(eng) < min(j, n_jobs):
-                emit(eng)
-
-        def w_quant(r):
-            regroup_upto("V", r + 1)
-            regroup_upto("S", r + 1)
-            width = jobs[r]["width"]
-            wc[r] = codp.tile([P, JW], U32, name="wc", tag="wc", align_bytes=64)
-            ws[r] = codp.tile([P, JW], U8, name="ws", tag="ws", align_bytes=64)
-            for s0, s1 in QSPLIT.get(r, [(0, len(jobs[r]["segs"]))]):
-                a = s0 * width
-                b = s1 * width
-                quantise(wc[r][:, a:b], ws[r][:, a:b], grp[r][:, a:b, :], b - a)
-            done["quant"] = r + 1
+        def w_quant(u):
+            wc[u] = codp.tile([P, W], U32, name="wc", tag="wc", align_bytes=64)
+            ws[u] = codp.tile([P, W], U8, name="ws", tag="ws", align_bytes=64)
+            if u == 31:
+                for a in (0, HALF):
+                    nc.vector.quantize_mx(
+                        out=wc[u][:, a : a + HALF].bitcast(FP8X4),
+                        scales=ws[u][:, a : a + HALF],
+                        in_=grp[u][:, a : a + HALF, :].rearrange("p w t -> p (w t)"),
+                    )
+            else:
+                quantise(wc[u][:], ws[u][:], grp[u])
 
         slot = {0: 0, 2: 1, 3: 2, 1: 3}
         junk = const.tile([P, D], BF16, name="junk")
         sum1 = const.tile([P, 1], F32, name="sum1")
         negmu1 = const.tile([P, 1], F32, name="negmu1")
         ssq1 = const.tile([P, 1], F32, name="ssq1")
-        nc.scalar.activation(out=junk[:], in_=x_all[:, 1, :], func=ACT.Identity, accum_out=sum1[:])
+        nc.scalar.activation(out=junk[:], in_=x_sb[1][:], func=ACT.Identity, accum_out=sum1[:])
         nc.scalar.mul(out=negmu1[:], in_=sum1[:], mul=-1.0 / D)
         nc.scalar.activation(
-            out=junk[:], in_=x_all[:, 1, :], func=ACT.Square, bias=negmu1[:, 0:1], scale=1.0,
+            out=junk[:], in_=x_sb[1][:], func=ACT.Square, bias=negmu1[:, 0:1], scale=1.0,
             accum_out=ssq1[:],
         )
 
@@ -236,7 +191,7 @@ def tile_layernormmlp_kernel(
         for i in (0, 2, 3):
             for s in range(2):
                 nc.vector.bn_stats(
-                    out=stats[:, slot[i], s, :], in_=x_all[:, i, s * 512 : (s + 1) * 512]
+                    out=stats[:, slot[i], s, :], in_=x_sb[i][:, s * 512 : (s + 1) * 512]
                 )
             nc.vector.bn_aggr(
                 out=mv[:, slot[i], :], in_=stats[:, slot[i], :, :].rearrange("p s k -> p (s k)")
@@ -244,12 +199,7 @@ def tile_layernormmlp_kernel(
             if i == 0:
                 nc.vector.tensor_copy(out=vec_t[:], in_=vt_ps[:, 0:48])
 
-        negmean = const.tile([P, 4], F32, name="negmean")
-        nc.vector.tensor_scalar(
-            out=negmean[:, 0:3], in0=mv[:, :, 0], scalar1=-1.0, scalar2=None, op0=ALU.mult
-        )
-        nc.vector.tensor_copy(out=negmean[:, 3:4], in_=negmu1[:])
-        run_seq("S", S_SEQ[0])
+        regroup_s(S_PRE[0])
         std = const.tile([P, 4], F32, name="std")
         nc.scalar.activation(
             out=std[:, 3:4], in_=ssq1[:], func=ACT.Sqrt, bias=eps_t[:, 0:1], scale=1.0 / D
@@ -257,48 +207,37 @@ def tile_layernormmlp_kernel(
         nc.scalar.activation(
             out=std[:, 0:3], in_=mv[:, :, 1], func=ACT.Sqrt, bias=eps_t[:, 0:1], scale=1.0
         )
-        run_seq("V", V_SEQ[0])
+        regroup_v(V_PRE[0])
         rstd = const.tile([P, 4], F32, name="rstd")
         nc.vector.reciprocal(out=rstd[:], in_=std[:])
-        nmr = const.tile([P, 4], F32, name="nmr")
-        nc.vector.tensor_tensor(out=nmr[:], in0=negmean[:], in1=rstd[:], op=ALU.mult)
-        run_seq("S", S_SEQ[1])
 
         ln_ps = []
         for b in range(8):
             ln_b = psum.tile([P, T], F32, name="ln_ps%d" % b, tag="bank%d" % b)
             ln_ps.append(ln_b)
-        xh = []
-        for half in range(2):
-            xh_h = ring.tile([P, 2, D], F32, name="xh", tag="ring")
-            xh.append(xh_h)
         for i in range(4):
-            xh_i = xh[i // 2][:, i % 2, :]
-            s = slot[i]
-            if XH_ON[i] == "S":
-                nc.scalar.activation(
-                    out=xh_i, in_=x_all[:, i, :], func=ACT.Identity,
-                    scale=rstd[:, s : s + 1], bias=nmr[:, s : s + 1],
+            xh = const.tile([P, D], F32, name="xh%d" % i)
+            if i == 1:
+                nc.vector.tensor_scalar(
+                    out=xh[:], in0=x_sb[i][:], scalar1=negmu1[:, 0:1], scalar2=rstd[:, 3:4],
+                    op0=ALU.add, op1=ALU.mult,
                 )
             else:
                 nc.vector.tensor_scalar(
-                    out=xh_i, in0=x_all[:, i, :], scalar1=negmean[:, s : s + 1],
-                    scalar2=rstd[:, s : s + 1], op0=ALU.add, op1=ALU.mult,
+                    out=xh[:], in0=x_sb[i][:], scalar1=mv[:, slot[i], 0:1],
+                    scalar2=rstd[:, slot[i] : slot[i] + 1], op0=ALU.subtract, op1=ALU.mult,
                 )
             for b in range(8):
                 nc.tensor.transpose(
-                    ln_ps[b][:, i * P : (i + 1) * P], xh_i[:, b * P : (b + 1) * P], ident_f[:]
+                    ln_ps[b][:, i * P : (i + 1) * P], xh[:, b * P : (b + 1) * P], ident_f[:]
                 )
-        lnp = ring.tile([P, 8, T], BF16, name="lnp", tag="ring")
-        done["free"] = 3
-        refill()
         nc.scalar.activation(out=warm[:, 1:2], in_=std[:, 0:1], func=ACT.Gelu_apprx_tanh)
-        run_seq("S", S_SEQ[2])
-        run_seq("V", V_SEQ[1])
-        refill()
+        regroup_s(S_PRE[1])
+        regroup_v(V_PRE[1])
 
-        for b in EV_ORDER:
-            if EV_ON[b] == "S":
+        lnp = const.tile([P, 8, T], BF16, name="lnp")
+        for b in (0, 2, 1, 3, 4, 6, 5, 7):
+            if b % 4 < 2:
                 nc.scalar.activation(
                     out=lnp[:, b, :], in_=ln_ps[b][:], func=ACT.Identity,
                     scale=vec_t[:, b : b + 1], bias=vec_t[:, 8 + b : 9 + b],
@@ -308,21 +247,18 @@ def tile_layernormmlp_kernel(
                     out=lnp[:, b, :], in0=ln_ps[b][:], scalar1=vec_t[:, b : b + 1],
                     scalar2=vec_t[:, 8 + b : 9 + b], op0=ALU.mult, op1=ALU.add,
                 )
-        lnc = const.tile([P, 2 * T], U32, name="lnc", align_bytes=64)
-        lns = const.tile([P, 2 * T], U8, name="lns", align_bytes=64)
-        lng = grpp.tile([P, JW, 4], BF16, name="grp", tag="grp", align_bytes=64)
+        lnc = const.tile([P, 2, T], U32, name="lnc", align_bytes=64)
+        lns = const.tile([P, 2, T], U8, name="lns", align_bytes=64)
+        lng = []
         for g in range(2):
-            regroup_part(
-                nc.vector.tensor_copy, lng[:, g * T : (g + 1) * T, :], lnp[:, 4 * g : 4 * g + 4, :]
-            )
-        done["free"] = 4
-        refill()
-        run_seq("V", V_SEQ[2])
-        refill()
-        quantise(lnc[:], lns[:], lng[:], 2 * T)
+            lng_g = grpp.tile([P, W, 4], BF16, name="grp", tag="grp", align_bytes=64)
+            regroup_part(nc.vector.tensor_copy, lng_g, lnp[:, 4 * g : 4 * g + 4, :], 0, W)
+            lng.append(lng_g)
+        for g in range(2):
+            quantise(lnc[:, g, :], lns[:, g, :], lng[g])
 
-        hc = const.tile([P, 8 * T], U32, name="hc", align_bytes=64)
-        hs = const.tile([P, 8 * T], U8, name="hs", align_bytes=64)
+        hc = const.tile([P, 8, T], U32, name="hc", align_bytes=64)
+        hs = const.tile([P, 8, T], U8, name="hs", align_bytes=64)
         acc1 = {}
         acc2 = {}
         hp = {}
@@ -332,20 +268,20 @@ def tile_layernormmlp_kernel(
             for j in range(4):
                 acc = psum.tile([P, T], F32, name="acc1", tag="bank%d" % ((4 * q + j) % 8))
                 for c in range(2):
-                    a = c * 512 + j * P
+                    u = 2 * q + c
                     nc.tensor.matmul_mx(
                         out=acc[:],
-                        lhsT=wc[q][:, a : a + P].bitcast(FP8X4),
-                        lhsT_scale=ws[q][:, a : a + P],
-                        rhs=lnc[:, c * T : (c + 1) * T].bitcast(FP8X4),
-                        rhs_scale=lns[:, c * T : (c + 1) * T],
+                        lhsT=wc[u][:, j * P : (j + 1) * P].bitcast(FP8X4),
+                        lhsT_scale=ws[u][:, j * P : (j + 1) * P],
+                        rhs=lnc[:, c, :].bitcast(FP8X4),
+                        rhs_scale=lns[:, c, :],
                         start=(c == 0),
                         stop=(c == 1),
                     )
                 acc1[(q, j)] = acc
 
         def gelu(q):
-            hp[q] = hpp.tile([P, 4, T], BF16, name="hp", tag="hp")
+            hp[q] = hidp.tile([P, 4, T], BF16, name="hp", tag="hp")
             for j in range(4):
                 nc.scalar.activation(
                     out=hp[q][:, j, :], in_=acc1[(q, j)][:], func=ACT.Gelu_apprx_tanh,
@@ -353,72 +289,60 @@ def tile_layernormmlp_kernel(
                 )
 
         def h_regroup(q):
-            if q % 2 == 0:
-                hg[q // 2] = hgp.tile([P, JW, 4], BF16, name="hg", tag="hg", align_bytes=64)
-            regroup_part(
-                nc.vector.tensor_copy, hg[q // 2][:, (q % 2) * T : (q % 2 + 1) * T, :], hp[q][:]
-            )
+            hg[q] = hidp.tile([P, W, 4], BF16, name="hg", tag="hg", align_bytes=64)
+            regroup_part(nc.vector.tensor_copy, hg[q], hp[q][:], 0, W)
 
         def h_quant(q):
-            if q % 2 == 1:
-                a = (q - 1) * T
-                quantise(hc[:, a : a + 2 * T], hs[:, a : a + 2 * T], hg[q // 2][:], 2 * T)
+            quantise(hc[:, q, :], hs[:, q, :], hg[q])
 
-        def fc2(r):
-            job = jobs[r]
-            width = job["width"]
-            bi = job["block"]
-            for si in range(len(job["segs"])):
-                g = job["segs"][si][1]
+        def fc2(u):
+            blk = 0 if u < 24 else 1 + (u - 24) // 4
+            off = 0
+            for g, src, width in unit_segs(u):
                 for i in range(4):
                     if g == 0:
-                        acc2[(bi, i)] = psum.tile(
-                            [P, width], F32, name="acc2", tag="bank%d" % (4 * (bi % 2) + i)
+                        acc2[(blk, i)] = psum.tile(
+                            [P, width], F32, name="acc2", tag="bank%d" % (4 * (blk % 2) + i)
                         )
-                    a = g * T + i * P
                     nc.tensor.matmul_mx(
-                        out=acc2[(bi, i)][:],
-                        lhsT=hc[:, a : a + P].bitcast(FP8X4),
-                        lhsT_scale=hs[:, a : a + P],
-                        rhs=wc[r][:, si * width : (si + 1) * width].bitcast(FP8X4),
-                        rhs_scale=ws[r][:, si * width : (si + 1) * width],
+                        out=acc2[(blk, i)][:],
+                        lhsT=hc[:, g, i * P : (i + 1) * P].bitcast(FP8X4),
+                        lhsT_scale=hs[:, g, i * P : (i + 1) * P],
+                        rhs=wc[u][:, off : off + width].bitcast(FP8X4),
+                        rhs_scale=ws[u][:, off : off + width],
                         start=(g == 0),
                         stop=(g == 7),
                     )
+                off = off + width
 
-        def finish(bi):
-            c0, width = BLOCKS[bi]
+        def finish(blk):
+            c0, width = ((0, W), (W, HALF), (W + HALF, HALF))[blk]
             for i in range(4):
                 o_sb = outp.tile([P, width], F32, name="o_sb", tag="o_sb")
                 nc.vector.tensor_tensor(
-                    out=o_sb[:], in0=acc2[(bi, i)][:], in1=b2[:, c0 : c0 + width], op=ALU.add
+                    out=o_sb[:], in0=acc2[(blk, i)][:], in1=b2[:, c0 : c0 + width], op=ALU.add
                 )
                 nc.sync.dma_start(out=out[i * P : (i + 1) * P, c0 : c0 + width], in_=o_sb[:])
 
-        fin_at = {}
-        for ji, job in enumerate(jobs):
-            if job["kind"] == 2:
-                fin_at[job["block"]] = ji + FIN_DELAY
-
-        for r in range(n_jobs):
-            regroup_upto("S", r + 1 + LOOK_S)
-            regroup_upto("V", r + 1 + LOOK_V)
+        for r in range(16):
+            regroup_s(2 * r + 2 + LOOK_S)
+            regroup_v(2 * r + 2)
             refill()
-            if 0 <= r - DG < 8:
-                gelu(r - DG)
-            if 0 <= r - DH < 8:
-                h_regroup(r - DH)
-            if r >= done["quant"]:
-                w_quant(r)
-            if 0 <= r - DH < 8:
-                h_quant(r - DH)
+            if 2 <= r < 10:
+                h_regroup(r - 2)
+            w_quant(2 * r)
+            w_quant(2 * r + 1)
+            if 2 <= r < 10:
+                h_quant(r - 2)
             if r < 8:
                 fc1(r)
             else:
-                fc2(r)
-            for bi in range(len(BLOCKS)):
-                if fin_at[bi] == r:
-                    finish(bi)
-        for bi in range(len(BLOCKS)):
-            if fin_at[bi] >= n_jobs:
-                finish(bi)
+                fc2(2 * r)
+                fc2(2 * r + 1)
+            if 1 <= r < 9:
+                gelu(r - 1)
+            if r == 12:
+                finish(0)
+            if r == 14:
+                finish(1)
+        finish(2)

from contextlib import ExitStack

import concourse.mybir as mybir
from concourse.masks import make_identity

F32 = mybir.dt.float32
BF16 = mybir.dt.bfloat16
U32 = mybir.dt.uint32
U8 = mybir.dt.uint8
FP8X4 = mybir.dt.float8_e4m3fn_x4
ACT = mybir.ActivationFunctionType
ALU = mybir.AluOpType

P = 128
T = 512
D = 1024
F1 = 4096
F2 = 1024
EPS = 1e-3
FLOPS = 2 * T * D * F1 + 2 * T * F1 * F2

W = 512
HALF = 256
Q_COLS = 256
RAW_BUFS = 10
S_PIECE = 256
LOOK_S = 2
V_COLS = [272,288,128,128,256,256,368,368,368,368,256,256,256,256,256,256,216,216,216,216,0,168,200,200,256,256,0,128,256,256,128,0]
S_PRE = (1, 3)
V_PRE = (1, 2)
PINNED = True


def tile_layernormmlp_kernel(
    tc, inputs, gamma, beta, fc1_kernel, fc1_bias, fc2_kernel, fc2_bias, out
):
    nc = tc.nc
    with ExitStack() as ctx:
        const = ctx.enter_context(tc.tile_pool(name="const", bufs=1))
        rawp = ctx.enter_context(tc.tile_pool(name="rawp", bufs=RAW_BUFS))
        grpp = ctx.enter_context(tc.tile_pool(name="grpp", bufs=8))
        codp = ctx.enter_context(tc.tile_pool(name="codp", bufs=6))
        hidp = ctx.enter_context(tc.tile_pool(name="hidp", bufs=3))
        outp = ctx.enter_context(tc.tile_pool(name="outp", bufs=4))
        psum = ctx.enter_context(tc.psum_pool(name="psum", bufs=1))
        if PINNED:
            ctx.enter_context(tc.manual_schedule())

        def regroup_part(copy_fn, dst, src, lo, hi):
            copy_fn(
                out=dst[:, lo:hi, :].rearrange("p (c i) t -> p c t i", i=4),
                in_=src[:, :, lo:hi].rearrange("p t (c i) -> p c t i", i=4),
            )

        def quantise(codes, scales, grouped):
            for a in range(0, W, Q_COLS):
                nc.vector.quantize_mx(
                    out=codes[:, a : a + Q_COLS].bitcast(FP8X4),
                    scales=scales[:, a : a + Q_COLS],
                    in_=grouped[:, a : a + Q_COLS, :].rearrange("p w t -> p (w t)"),
                )

        ident_b = const.tile([P, P], BF16, name="ident_b")
        make_identity(nc, ident_b[:])
        ident_f = const.tile([P, P], F32, name="ident_f")
        make_identity(nc, ident_f[:])
        eps_t = const.tile([P, 1], F32, name="eps_t")
        nc.vector.memset(eps_t[:], EPS)
        vec = const.tile([P, P], BF16, name="vec")
        nc.vector.memset(vec[:], 0.0)

        x_sb = []
        for i in range(4):
            x_i = const.tile([P, D], BF16, name="x%d" % i)
            nc.sync.dma_start(out=x_i[:], in_=inputs[i * P : (i + 1) * P, :])
            x_sb.append(x_i)
        nc.scalar.dma_start(out=vec[0:8, :], in_=gamma.rearrange("(r c) -> r c", c=P))
        nc.scalar.dma_start(out=vec[8:16, :], in_=beta.rearrange("(r c) -> r c", c=P))
        nc.scalar.dma_start(out=vec[16:48, :], in_=fc1_bias.rearrange("(r c) -> r c", c=P))
        warm = const.tile([P, 2], F32, name="warm")
        nc.scalar.activation(out=warm[:, 0:1], in_=eps_t[:], func=ACT.Sqrt)

        raw = {}

        def load(k):
            if k < 8:
                t = rawp.tile([P, 8, W], BF16, name="raw", tag="raw")
                view = fc1_kernel[:, k * W : (k + 1) * W].rearrange("(a p) f -> p a f", p=P)
                if k == 0:
                    nc.sync.dma_start(out=t[:, 0:4, :], in_=view[:, 0:4, :])
                    nc.sync.dma_start(out=t[:, 4:8, :], in_=view[:, 4:8, :])
                else:
                    nc.sync.dma_start(out=t[:], in_=view)
            else:
                g = k - 8
                t = rawp.tile([P, 4, F2], BF16, name="raw", tag="raw")
                nc.sync.dma_start(
                    out=t[:],
                    in_=fc2_kernel[g * 512 : (g + 1) * 512, :].rearrange("(a p) n -> p a n", p=P),
                )
            raw[k] = t

        for k in range(RAW_BUFS):
            load(k)
        b2 = const.tile([P, F2], BF16, name="b2")
        nc.sync.dma_start(out=b2[:], in_=fc2_bias.partition_broadcast(P))

        grp = {}
        wc = {}
        ws = {}
        nxt = {"S": 0, "V": 0, "load": RAW_BUFS}

        def unit_segs(u):
            if u < 16:
                return [(None, raw[u // 2][:, 4 * (u % 2) : 4 * (u % 2) + 4, :], W)]
            if u < 24:
                return [(u - 16, raw[8 + u - 16][:, :, 0:W], W)]
            c0 = W + HALF * ((u - 24) // 4)
            g0 = 2 * ((u - 24) % 4)
            return [(g, raw[8 + g][:, :, c0 : c0 + HALF], HALF) for g in (g0, g0 + 1)]

        def regroup_range(copy_fn, u, lo, hi):
            off = 0
            for g, src, width in unit_segs(u):
                a = max(lo, off)
                b = min(hi, off + width)
                if b > a:
                    copy_fn(
                        out=grp_tile(u)[:, a:b, :].rearrange("p (c i) t -> p c t i", i=4),
                        in_=src[:, :, a - off : b - off].rearrange("p t (c i) -> p c t i", i=4),
                    )
                off = off + width

        def grp_tile(u):
            if u not in grp:
                grp[u] = grpp.tile([P, W, 4], BF16, name="grp", tag="grp", align_bytes=64)
            return grp[u]

        def regroup_s(upto):
            while nxt["S"] < min(upto, 32):
                u = nxt["S"]
                lo = V_COLS[u]
                while lo < W:
                    hi = min(W, lo + S_PIECE) if u < 24 else min(W, (lo // HALF + 1) * HALF)
                    regroup_range(nc.scalar.copy, u, lo, hi)
                    lo = hi
                nxt["S"] = u + 1

        def regroup_v(upto):
            while nxt["V"] < min(upto, 32):
                u = nxt["V"]
                if V_COLS[u] > 0:
                    regroup_range(nc.vector.tensor_copy, u, 0, V_COLS[u])
                nxt["V"] = u + 1

        def refill():
            while nxt["load"] < 16 and (nxt["load"] - RAW_BUFS) * 2 + 2 <= min(nxt["S"], nxt["V"]):
                load(nxt["load"])
                nxt["load"] = nxt["load"] + 1

        def w_quant(u):
            wc[u] = codp.tile([P, W], U32, name="wc", tag="wc", align_bytes=64)
            ws[u] = codp.tile([P, W], U8, name="ws", tag="ws", align_bytes=64)
            if u == 31:
                for a in (0, HALF):
                    nc.vector.quantize_mx(
                        out=wc[u][:, a : a + HALF].bitcast(FP8X4),
                        scales=ws[u][:, a : a + HALF],
                        in_=grp[u][:, a : a + HALF, :].rearrange("p w t -> p (w t)"),
                    )
            else:
                quantise(wc[u][:], ws[u][:], grp[u])

        slot = {0: 0, 2: 1, 3: 2, 1: 3}
        junk = const.tile([P, D], BF16, name="junk")
        sum1 = const.tile([P, 1], F32, name="sum1")
        negmu1 = const.tile([P, 1], F32, name="negmu1")
        ssq1 = const.tile([P, 1], F32, name="ssq1")
        nc.scalar.activation(out=junk[:], in_=x_sb[1][:], func=ACT.Identity, accum_out=sum1[:])
        nc.scalar.mul(out=negmu1[:], in_=sum1[:], mul=-1.0 / D)
        nc.scalar.activation(
            out=junk[:], in_=x_sb[1][:], func=ACT.Square, bias=negmu1[:, 0:1], scale=1.0,
            accum_out=ssq1[:],
        )

        stats = const.tile([P, 3, 2, 6], F32, name="stats")
        mv = const.tile([P, 3, 2], F32, name="mv")
        vt_ps = psum.tile([P, P], BF16, name="vt_ps", tag="bank0")
        nc.tensor.transpose(vt_ps[:], vec[:], ident_b[:])
        vec_t = const.tile([P, 48], F32, name="vec_t")
        for i in (0, 2, 3):
            for s in range(2):
                nc.vector.bn_stats(
                    out=stats[:, slot[i], s, :], in_=x_sb[i][:, s * 512 : (s + 1) * 512]
                )
            nc.vector.bn_aggr(
                out=mv[:, slot[i], :], in_=stats[:, slot[i], :, :].rearrange("p s k -> p (s k)")
            )
            if i == 0:
                nc.vector.tensor_copy(out=vec_t[:], in_=vt_ps[:, 0:48])

        regroup_s(S_PRE[0])
        std = const.tile([P, 4], F32, name="std")
        nc.scalar.activation(
            out=std[:, 3:4], in_=ssq1[:], func=ACT.Sqrt, bias=eps_t[:, 0:1], scale=1.0 / D
        )
        nc.scalar.activation(
            out=std[:, 0:3], in_=mv[:, :, 1], func=ACT.Sqrt, bias=eps_t[:, 0:1], scale=1.0
        )
        regroup_v(V_PRE[0])
        rstd = const.tile([P, 4], F32, name="rstd")
        nc.vector.reciprocal(out=rstd[:], in_=std[:])

        ln_ps = []
        for b in range(8):
            ln_b = psum.tile([P, T], F32, name="ln_ps%d" % b, tag="bank%d" % b)
            ln_ps.append(ln_b)
        for i in range(4):
            xh = const.tile([P, D], F32, name="xh%d" % i)
            if i == 1:
                nc.vector.tensor_scalar(
                    out=xh[:], in0=x_sb[i][:], scalar1=negmu1[:, 0:1], scalar2=rstd[:, 3:4],
                    op0=ALU.add, op1=ALU.mult,
                )
            else:
                nc.vector.tensor_scalar(
                    out=xh[:], in0=x_sb[i][:], scalar1=mv[:, slot[i], 0:1],
                    scalar2=rstd[:, slot[i] : slot[i] + 1], op0=ALU.subtract, op1=ALU.mult,
                )
            for b in range(8):
                nc.tensor.transpose(
                    ln_ps[b][:, i * P : (i + 1) * P], xh[:, b * P : (b + 1) * P], ident_f[:]
                )
        nc.scalar.activation(out=warm[:, 1:2], in_=std[:, 0:1], func=ACT.Gelu_apprx_tanh)
        regroup_s(S_PRE[1])
        regroup_v(V_PRE[1])

        lnp = const.tile([P, 8, T], BF16, name="lnp")
        for b in (0, 2, 1, 3, 4, 6, 5, 7):
            if b % 4 < 2:
                nc.scalar.activation(
                    out=lnp[:, b, :], in_=ln_ps[b][:], func=ACT.Identity,
                    scale=vec_t[:, b : b + 1], bias=vec_t[:, 8 + b : 9 + b],
                )
            else:
                nc.vector.tensor_scalar(
                    out=lnp[:, b, :], in0=ln_ps[b][:], scalar1=vec_t[:, b : b + 1],
                    scalar2=vec_t[:, 8 + b : 9 + b], op0=ALU.mult, op1=ALU.add,
                )
        lnc = const.tile([P, 2, T], U32, name="lnc", align_bytes=64)
        lns = const.tile([P, 2, T], U8, name="lns", align_bytes=64)
        lng = []
        for g in range(2):
            lng_g = grpp.tile([P, W, 4], BF16, name="grp", tag="grp", align_bytes=64)
            regroup_part(nc.vector.tensor_copy, lng_g, lnp[:, 4 * g : 4 * g + 4, :], 0, W)
            lng.append(lng_g)
        for g in range(2):
            quantise(lnc[:, g, :], lns[:, g, :], lng[g])

        hc = const.tile([P, 8, T], U32, name="hc", align_bytes=64)
        hs = const.tile([P, 8, T], U8, name="hs", align_bytes=64)
        acc1 = {}
        acc2 = {}
        hp = {}
        hg = {}

        def fc1(q):
            for j in range(4):
                acc = psum.tile([P, T], F32, name="acc1", tag="bank%d" % ((4 * q + j) % 8))
                for c in range(2):
                    u = 2 * q + c
                    nc.tensor.matmul_mx(
                        out=acc[:],
                        lhsT=wc[u][:, j * P : (j + 1) * P].bitcast(FP8X4),
                        lhsT_scale=ws[u][:, j * P : (j + 1) * P],
                        rhs=lnc[:, c, :].bitcast(FP8X4),
                        rhs_scale=lns[:, c, :],
                        start=(c == 0),
                        stop=(c == 1),
                    )
                acc1[(q, j)] = acc

        def gelu(q):
            hp[q] = hidp.tile([P, 4, T], BF16, name="hp", tag="hp")
            for j in range(4):
                nc.scalar.activation(
                    out=hp[q][:, j, :], in_=acc1[(q, j)][:], func=ACT.Gelu_apprx_tanh,
                    bias=vec_t[:, 16 + 4 * q + j : 17 + 4 * q + j], scale=1.0,
                )

        def h_regroup(q):
            hg[q] = hidp.tile([P, W, 4], BF16, name="hg", tag="hg", align_bytes=64)
            regroup_part(nc.vector.tensor_copy, hg[q], hp[q][:], 0, W)

        def h_quant(q):
            quantise(hc[:, q, :], hs[:, q, :], hg[q])

        def fc2(u):
            blk = 0 if u < 24 else 1 + (u - 24) // 4
            off = 0
            for g, src, width in unit_segs(u):
                for i in range(4):
                    if g == 0:
                        acc2[(blk, i)] = psum.tile(
                            [P, width], F32, name="acc2", tag="bank%d" % (4 * (blk % 2) + i)
                        )
                    nc.tensor.matmul_mx(
                        out=acc2[(blk, i)][:],
                        lhsT=hc[:, g, i * P : (i + 1) * P].bitcast(FP8X4),
                        lhsT_scale=hs[:, g, i * P : (i + 1) * P],
                        rhs=wc[u][:, off : off + width].bitcast(FP8X4),
                        rhs_scale=ws[u][:, off : off + width],
                        start=(g == 0),
                        stop=(g == 7),
                    )
                off = off + width

        def finish(blk):
            c0, width = ((0, W), (W, HALF), (W + HALF, HALF))[blk]
            for i in range(4):
                o_sb = outp.tile([P, width], F32, name="o_sb", tag="o_sb")
                nc.vector.tensor_tensor(
                    out=o_sb[:], in0=acc2[(blk, i)][:], in1=b2[:, c0 : c0 + width], op=ALU.add
                )
                nc.sync.dma_start(out=out[i * P : (i + 1) * P, c0 : c0 + width], in_=o_sb[:])

        for r in range(16):
            regroup_s(2 * r + 2 + LOOK_S)
            regroup_v(2 * r + 2)
            refill()
            if 2 <= r < 10:
                h_regroup(r - 2)
            w_quant(2 * r)
            w_quant(2 * r + 1)
            if 2 <= r < 10:
                h_quant(r - 2)
            if r < 8:
                fc1(r)
            else:
                fc2(2 * r)
                fc2(2 * r + 1)
            if 1 <= r < 9:
                gelu(r - 1)
            if r == 12:
                finish(0)
            if r == 14:
                finish(1)
        finish(2)
